import numpy as np
import ml_dtypes


def mxq(x, axis, fmt="e4m3"):
    dtype, down = {"e4m3": (ml_dtypes.float8_e4m3fn, 7), "e5m2": (ml_dtypes.float8_e5m2, 14)}[fmt]
    v = np.moveaxis(np.asarray(x, np.float32).astype(ml_dtypes.bfloat16).astype(np.float64), axis, -1)
    blocks = v.reshape(v.shape[:-1] + (-1, 32))
    amax = np.abs(blocks).max(-1, keepdims=True)
    byte = np.maximum(np.where(amax > 0, np.frexp(amax)[1] - 1 + 127, 0) - down, 1)
    scale = np.exp2(byte - 127.0)
    codes = (blocks / scale).astype(np.float32).astype(dtype).astype(np.float64)
    return np.moveaxis((codes * scale).reshape(v.shape), -1, axis)


WIDE = False


def mx_kscale(k):
    if not WIDE:
        return np.ones(k)
    levels = np.array([10, -10, 5, -5, 0])
    a = np.random.permutation(np.resize(levels, k // 512 * 4)).reshape(k // 512, 4)
    idx = np.arange(k)
    return np.exp2(a[idx // 512, idx % 128 // 32])


BF16 = ml_dtypes.bfloat16


def bf(x):
    return np.asarray(x, np.float32).astype(BF16)


def f64(x):
    return np.asarray(x).astype(np.float64)


NQ, NK, QS, KS, F, DEG = 1024, 1024, 512, 512, 512, 32


def setup_inputs():
    s = mx_kscale(F)
    return {"A": bf(np.random.random((NQ, NK)) < DEG / NK),
            "qe1": bf(np.random.standard_normal((NQ, F)) * s),
            "ke1": bf(np.random.standard_normal((NK, F)) / s),
            "ve1": bf(np.random.standard_normal((NK, F)) * 2.0)}


def reference(A, qe1, ke1, ve1):
    prod = (mxq(f64(qe1), 1, "e4m3") @ mxq(f64(ke1), 1, "e4m3").T) / np.sqrt(F)
    masked = f64(A) * prod
    e = np.exp(masked - masked.max(axis=1, keepdims=True))
    return (mxq(e, 1, "e4m3") @ mxq(f64(ve1), 0, "e4m3")) / e.sum(axis=1, keepdims=True)

@@ -1,0 +1,357 @@
+from contextlib import ExitStack
+import math
+
+import concourse.mybir as mybir
+from concourse.masks import make_identity
+
+FP8X4 = mybir.dt.float8_e4m3fn_x4
+BF16 = mybir.dt.bfloat16
+F32 = mybir.dt.float32
+U32 = mybir.dt.uint32
+U8 = mybir.dt.uint8
+ALU = mybir.AluOpType
+ACT = mybir.ActivationFunctionType
+
+P = 128
+NQ = 1024
+NK = 1024
+F = 512
+QT = NQ // P
+FLOPS = 2 * NQ * NK * F * 2
+INV_SQRT_F = 1.0 / math.sqrt(F)
+
+
+def tile_attention_prop_pb_kernel(tc, A, qe1, ke1, ve1, out):
+    nc = tc.nc
+    with ExitStack() as ctx:
+        keep = ctx.enter_context(tc.tile_pool(name="keep", bufs=1))
+        pools = {
+            "s": ctx.enter_context(tc.psum_pool(name="ps_s", bufs=3)),
+            "t": ctx.enter_context(tc.psum_pool(name="ps_t", bufs=3)),
+            "o": ctx.enter_context(tc.psum_pool(name="ps_o", bufs=2)),
+        }
+        ctx.enter_context(tc.manual_schedule())
+
+        ident_f = keep.tile([P, P], F32, name="ident_f")
+        make_identity(nc, ident_f[:])
+        ident_b = keep.tile([P, P], BF16, name="ident_b")
+        make_identity(nc, ident_b[:])
+
+        k_view = ke1.rearrange("(j p) f -> p j f", p=P)
+        q_view = qe1.rearrange("(p i) f -> p i f", i=QT)
+        a_view = A.rearrange("(p i) k -> p i k", i=QT)
+        v_view = ve1.rearrange("(b p) f -> p b f", p=P)
+        o_view = out.rearrange("(p i) f -> p i f", i=QT)
+
+        qraw = [keep.tile([P, 2, F], BF16, name="qraw%d" % a) for a in range(4)]
+        kraw = [keep.tile([P, 2, F], BF16, name="kraw%d" % a) for a in range(4)]
+        araw = [keep.tile([P, 2, NK], BF16, name="araw%d" % a) for a in range(4)]
+        vraw = [keep.tile([P, 4, F], BF16, name="vraw%d" % c) for c in range(2)]
+        qgrp = keep.tile([P, NQ * 4], BF16, name="qgrp", align_bytes=64)
+        kgrp = keep.tile([P, NK * 4], BF16, name="kgrp", align_bytes=64)
+        vgrp = keep.tile([P, 2, F, 4], BF16, name="vgrp", align_bytes=64)
+        qcodes = keep.tile([P, NQ], U32, name="qcodes", align_bytes=64)
+        kcodes = keep.tile([P, NK], U32, name="kcodes", align_bytes=64)
+        vcodes = keep.tile([P, 2 * F], U32, name="vcodes", align_bytes=64)
+        qscl = keep.tile([P, NQ], U8, name="qscl", align_bytes=64)
+        kscl = keep.tile([P, NK], U8, name="kscl", align_bytes=64)
+        vscl = keep.tile([P, 2 * F], U8, name="vscl", align_bytes=64)
+        m = [keep.tile([P, NK], F32, name="m%d" % i) for i in range(QT)]
+        e = [keep.tile([P, NK], BF16, name="e%d" % i) for i in range(QT)]
+        egrp = [keep.tile([P, 2, P, 4], BF16, name="egrp%d" % i, align_bytes=64) for i in range(QT)]
+        ecodes = [keep.tile([P, 2 * P], U32, name="ecodes%d" % i, align_bytes=64) for i in range(QT)]
+        escl = [keep.tile([P, 2 * P], U8, name="escl%d" % i, align_bytes=64) for i in range(QT)]
+        o_sb = [keep.tile([P, F], F32, name="o_sb%d" % i) for i in range(QT)]
+        nmax = [keep.tile([P, 1], F32, name="nmax%d" % i) for i in range(QT)]
+        esum = [keep.tile([P, 1], F32, name="esum%d" % i) for i in range(QT)]
+        rsum = [keep.tile([P, 1], F32, name="rsum%d" % i) for i in range(QT)]
+        ps = {}
+
+        def LQ(a):
+            nc.sync.dma_start(out=qraw[a][:], in_=q_view[:, 2 * a:2 * a + 2, :])
+
+        def LK(a):
+            nc.sync.dma_start(out=kraw[a][:], in_=k_view[:, 2 * a:2 * a + 2, :])
+
+        def LA(a):
+            nc.sync.dma_start(out=araw[a][:], in_=a_view[:, 2 * a:2 * a + 2, :])
+
+        def LV(c):
+            nc.sync.dma_start(out=vraw[c][:], in_=v_view[:, 4 * c:4 * c + 4, :])
+
+        def copy_on(eng, dst, src):
+            if eng == "S":
+                nc.scalar.copy(out=dst, in_=src)
+            else:
+                nc.vector.tensor_copy(out=dst, in_=src)
+
+        def flip(key, raw, tag):
+            xt = pools[tag].tile([P, 2, 2, P], F32, tag=tag, name="xt_" + key)
+            for j in range(2):
+                words = raw[:, j, :].bitcast(F32)
+                for u in range(2):
+                    nc.tensor.transpose(xt[:, j, u, :], words[:, u * P:(u + 1) * P], ident_f[:])
+            ps[key] = xt
+
+        def unflip(key, grp, a, eng):
+            dst = grp[:, a * 1024:(a + 1) * 1024].bitcast(F32).rearrange(
+                "p (j r u) -> p j r u", j=2, u=2)
+            copy_on(eng, dst, ps[key][:].rearrange("p j u r -> p j r u"))
+
+        def quantise(grp, codes, scl, lo, hi):
+            nc.vector.quantize_mx(
+                out=codes[:, lo:hi].bitcast(FP8X4), scales=scl[:, lo:hi], in_=grp[:, 4 * lo:4 * hi])
+
+        def TQ(a, tag="o"):
+            flip("q%d" % a, qraw[a], tag)
+
+        def evQ(a, eng):
+            unflip("q%d" % a, qgrp, a, eng)
+
+        def qQ(a):
+            quantise(qgrp, qcodes, qscl, 256 * a, 256 * (a + 1))
+
+        def TK(a, tag="t"):
+            flip("k%d" % a, kraw[a], tag)
+
+        def evK(a, eng):
+            unflip("k%d" % a, kgrp, a, eng)
+
+        def qK(h):
+            quantise(kgrp, kcodes, kscl, 512 * h, 512 * (h + 1))
+
+        def VR(c, eng):
+            src = vraw[c][:].rearrange("p t f -> p f t")
+            if eng == "G":
+                nc.gpsimd.tensor_scalar(
+                    out=vgrp[:, c, :, :], in0=src, scalar1=1.0, scalar2=0.0,
+                    op0=ALU.mult, op1=ALU.add)
+            else:
+                copy_on(eng, vgrp[:, c, :, :], src)
+
+        def VQ(c):
+            nc.vector.quantize_mx(
+                out=vcodes[:, c * F:(c + 1) * F].bitcast(FP8X4),
+                scales=vscl[:, c * F:(c + 1) * F],
+                in_=vgrp[:, c, :, :].rearrange("p f t -> p (f t)"))
+
+        def A_(i, h):
+            s = pools["s"].tile([P, 512], F32, tag="s", name="s%d_%d" % (i, h))
+            nc.tensor.matmul_mx(
+                out=s[:],
+                lhsT=qcodes[:, i * P:(i + 1) * P].bitcast(FP8X4),
+                lhsT_scale=qscl[:, i * P:(i + 1) * P],
+                rhs=kcodes[:, h * 512:(h + 1) * 512].bitcast(FP8X4),
+                rhs_scale=kscl[:, h * 512:(h + 1) * 512],
+                start=True, stop=True)
+            ps["s%d_%d" % (i, h)] = s
+
+        def M(i, h):
+            nc.vector.scalar_tensor_tensor(
+                out=m[i][:, h * 512:(h + 1) * 512],
+                in0=ps["s%d_%d" % (i, h)][:],
+                scalar=INV_SQRT_F,
+                in1=araw[i // 2][:, i % 2, h * 512:(h + 1) * 512],
+                op0=ALU.mult, op1=ALU.mult)
+
+        def X(i):
+            nc.vector.tensor_reduce(
+                out=nmax[i][:], in_=m[i][:], axis=mybir.AxisListType.X, op=ALU.max, negate=True)
+
+        def E(i):
+            nc.scalar.activation(
+                out=e[i][:], in_=m[i][:], func=ACT.Exp, bias=nmax[i][:], scale=1.0,
+                accum_out=esum[i][:])
+
+        def B(i, c):
+            et = pools["t"].tile([P, 4, P], BF16, tag="t", name="et%d_%d" % (i, c))
+            for t in range(4):
+                b = 4 * c + t
+                nc.tensor.transpose(et[:, t, :], e[i][:, b * P:(b + 1) * P], ident_b[:])
+            ps["et%d_%d" % (i, c)] = et
+
+        def G(i, c, eng="S"):
+            copy_on(eng, egrp[i][:, c, :, :], ps["et%d_%d" % (i, c)][:].rearrange("p t r -> p r t"))
+
+        def Qz(i):
+            nc.vector.quantize_mx(
+                out=ecodes[i][:].bitcast(FP8X4), scales=escl[i][:],
+                in_=egrp[i][:].rearrange("p c r t -> p (c r t)"))
+
+        def R(i):
+            nc.vector.reciprocal(rsum[i][:], esum[i][:])
+
+        def C(i):
+            o_ps = pools["o"].tile([P, F], F32, tag="o", name="o_ps%d" % i)
+            for c in range(2):
+                nc.tensor.matmul_mx(
+                    out=o_ps[:],
+                    lhsT=ecodes[i][:, c * P:(c + 1) * P].bitcast(FP8X4),
+                    lhsT_scale=escl[i][:, c * P:(c + 1) * P],
+                    rhs=vcodes[:, c * F:(c + 1) * F].bitcast(FP8X4),
+                    rhs_scale=vscl[:, c * F:(c + 1) * F],
+                    start=(c == 0), stop=(c == 1))
+            ps["o%d" % i] = o_ps
+
+        def O(i, eng="S"):
+            if eng == "S":
+                nc.scalar.activation(
+                    out=o_sb[i][:], in_=ps["o%d" % i][:], func=ACT.Copy, scale=rsum[i][:])
+            else:
+                nc.vector.tensor_scalar(
+                    out=o_sb[i][:], in0=ps["o%d" % i][:], scalar1=rsum[i][:], scalar2=None,
+                    op0=ALU.mult)
+            nc.sync.dma_start(out=o_view[:, i, :], in_=o_sb[i][:])
+
+        LQ(0)
+        LK(0)
+        LK(1)
+        LK(2)
+        LK(3)
+        LA(0)
+        LQ(1)
+        LQ(2)
+        LQ(3)
+        LA(1)
+        LV(0)
+        LV(1)
+        LA(2)
+        LA(3)
+        TQ(0)
+        evQ(0, "S")
+        qQ(0)
+        TK(0, "t")
+        evK(0, "V")
+        TK(1, "t")
+        evK(1, "S")
+        qK(0)
+        TK(2, "t")
+        evK(2, "V")
+        TK(3, "s")
+        evK(3, "S")
+        qK(1)
+        A_(0, 0)
+        A_(1, 0)
+        TQ(1)
+        evQ(1, "S")
+        TQ(2)
+        evQ(2, "S")
+        A_(0, 1)
+        VR(0, "G")
+        VR(1, "G")
+        M(0, 0)
+        A_(1, 1)
+        TQ(3)
+        evQ(3, "S")
+        M(1, 0)
+        M(0, 1)
+        X(0)
+        qQ(1)
+        A_(2, 0)
+        A_(2, 1)
+        M(1, 1)
+        A_(3, 0)
+        E(0)
+        B(0, 0)
+        B(0, 1)
+        X(1)
+        qQ(2)
+        E(1)
+        G(0, 0)
+        G(0, 1)
+        B(1, 0)
+        B(1, 1)
+        M(2, 0)
+        A_(3, 1)
+        M(2, 1)
+        A_(4, 0)
+        X(2)
+        qQ(3)
+        E(2)
+        G(1, 0)
+        G(1, 1)
+        B(2, 0)
+        B(2, 1)
+        M(3, 0)
+        A_(4, 1)
+        M(3, 1)
+        A_(5, 0)
+        X(3)
+        E(3)
+        G(2, 0)
+        G(2, 1)
+        B(3, 0)
+        B(3, 1)
+        M(4, 0)
+        A_(5, 1)
+        M(4, 1)
+        A_(6, 0)
+        X(4)
+        VQ(0)
+        VQ(1)
+        Qz(0)
+        R(0)
+        C(0)
+        E(4)
+        G(3, 0)
+        G(3, 1)
+        B(4, 0)
+        B(4, 1)
+        O(0, "S")
+        M(5, 0)
+        A_(6, 1)
+        M(5, 1)
+        A_(7, 0)
+        X(5)
+        Qz(1)
+        R(1)
+        C(1)
+        E(5)
+        G(4, 0)
+        G(4, 1)
+        B(5, 0)
+        B(5, 1)
+        O(1, "S")
+        M(6, 0)
+        A_(7, 1)
+        M(6, 1)
+        X(6)
+        Qz(2)
+        R(2)
+        C(2)
+        E(6)
+        G(5, 0)
+        G(5, 1)
+        B(6, 0)
+        B(6, 1)
+        O(2, "S")
+        M(7, 0)
+        M(7, 1)
+        X(7)
+        Qz(3)
+        Qz(4)
+        E(7)
+        C(3)
+        R(3)
+        G(6, 0, "V")
+        Qz(5)
+        C(4)
+        G(6, 1, "V")
+        O(3, "S")
+        B(7, 0)
+        R(4)
+        Qz(6)
+        B(7, 1)
+        O(4, "S")
+        C(5)
+        R(5)
+        G(7, 0, "V")
+        G(7, 1, "S")
+        C(6)
+        R(6)
+        R(7)
+        Qz(7)
+        O(5, "S")
+        O(6, "V")
+        C(7)
+        O(7, "S")

@@ -13,345 +13,215 @@ ALU = mybir.AluOpType
 ACT = mybir.ActivationFunctionType
 
 P = 128
+PACK = 4
 NQ = 1024
 NK = 1024
 F = 512
 QT = NQ // P
+HALF = 512
+PAIRS = 4
 FLOPS = 2 * NQ * NK * F * 2
 INV_SQRT_F = 1.0 / math.sqrt(F)
+
+SCORES_AHEAD = 3
+SECOND_STAGE_LAG = 3
+VECTOR_HELPS_FROM = QT - 2
 
 
 def tile_attention_prop_pb_kernel(tc, A, qe1, ke1, ve1, out):
     nc = tc.nc
     with ExitStack() as ctx:
-        keep = ctx.enter_context(tc.tile_pool(name="keep", bufs=1))
-        pools = {
-            "s": ctx.enter_context(tc.psum_pool(name="ps_s", bufs=3)),
-            "t": ctx.enter_context(tc.psum_pool(name="ps_t", bufs=3)),
-            "o": ctx.enter_context(tc.psum_pool(name="ps_o", bufs=2)),
-        }
+        sbuf = ctx.enter_context(tc.tile_pool(name="sbuf", bufs=1))
+        score_banks = ctx.enter_context(tc.psum_pool(name="score_banks", bufs=SCORES_AHEAD))
+        flip_banks = ctx.enter_context(tc.psum_pool(name="flip_banks", bufs=3))
+        out_banks = ctx.enter_context(tc.psum_pool(name="out_banks", bufs=2))
         ctx.enter_context(tc.manual_schedule())
 
-        ident_f = keep.tile([P, P], F32, name="ident_f")
-        make_identity(nc, ident_f[:])
-        ident_b = keep.tile([P, P], BF16, name="ident_b")
-        make_identity(nc, ident_b[:])
+        ident_f32 = sbuf.tile([P, P], F32, name="ident_f32")
+        make_identity(nc, ident_f32[:])
+        ident_bf16 = sbuf.tile([P, P], BF16, name="ident_bf16")
+        make_identity(nc, ident_bf16[:])
 
-        k_view = ke1.rearrange("(j p) f -> p j f", p=P)
+        q_raw = [sbuf.tile([P, 2, F], BF16, name="q_raw%d" % a) for a in range(PAIRS)]
+        k_raw = [sbuf.tile([P, 2, F], BF16, name="k_raw%d" % a) for a in range(PAIRS)]
+        a_raw = [sbuf.tile([P, 2, NK], BF16, name="a_raw%d" % a) for a in range(PAIRS)]
+        v_raw = [sbuf.tile([P, PACK, F], BF16, name="v_raw%d" % c) for c in range(2)]
+        q_grouped = sbuf.tile([P, NQ * PACK], BF16, name="q_grouped", align_bytes=64)
+        k_grouped = sbuf.tile([P, NK * PACK], BF16, name="k_grouped", align_bytes=64)
+        v_grouped = sbuf.tile([P, 2, F, PACK], BF16, name="v_grouped", align_bytes=64)
+        q_codes = sbuf.tile([P, NQ], U32, name="q_codes", align_bytes=64)
+        k_codes = sbuf.tile([P, NK], U32, name="k_codes", align_bytes=64)
+        v_codes = sbuf.tile([P, 2 * F], U32, name="v_codes", align_bytes=64)
+        q_scales = sbuf.tile([P, NQ], U8, name="q_scales", align_bytes=64)
+        k_scales = sbuf.tile([P, NK], U8, name="k_scales", align_bytes=64)
+        v_scales = sbuf.tile([P, 2 * F], U8, name="v_scales", align_bytes=64)
+        masked = [sbuf.tile([P, NK], F32, name="masked%d" % i) for i in range(QT)]
+        neg_max = [sbuf.tile([P, 1], F32, name="neg_max%d" % i) for i in range(QT)]
+        e_rows = [sbuf.tile([P, NK], BF16, name="e_rows%d" % i) for i in range(QT)]
+        e_sum = [sbuf.tile([P, 1], F32, name="e_sum%d" % i) for i in range(QT)]
+        e_grouped = [
+            sbuf.tile([P, 2, P, PACK], BF16, name="e_grouped%d" % i, align_bytes=64) for i in range(QT)]
+        e_codes = [sbuf.tile([P, 2 * P], U32, name="e_codes%d" % i, align_bytes=64) for i in range(QT)]
+        e_scales = [sbuf.tile([P, 2 * P], U8, name="e_scales%d" % i, align_bytes=64) for i in range(QT)]
+        inv_sum = [sbuf.tile([P, 1], F32, name="inv_sum%d" % i) for i in range(QT)]
+        result = [sbuf.tile([P, F], F32, name="result%d" % i) for i in range(QT)]
+        in_psum = {}
+
         q_view = qe1.rearrange("(p i) f -> p i f", i=QT)
+        k_view = ke1.rearrange("(j p) f -> p j f", p=P)
         a_view = A.rearrange("(p i) k -> p i k", i=QT)
         v_view = ve1.rearrange("(b p) f -> p b f", p=P)
         o_view = out.rearrange("(p i) f -> p i f", i=QT)
 
-        qraw = [keep.tile([P, 2, F], BF16, name="qraw%d" % a) for a in range(4)]
-        kraw = [keep.tile([P, 2, F], BF16, name="kraw%d" % a) for a in range(4)]
-        araw = [keep.tile([P, 2, NK], BF16, name="araw%d" % a) for a in range(4)]
-        vraw = [keep.tile([P, 4, F], BF16, name="vraw%d" % c) for c in range(2)]
-        qgrp = keep.tile([P, NQ * 4], BF16, name="qgrp", align_bytes=64)
-        kgrp = keep.tile([P, NK * 4], BF16, name="kgrp", align_bytes=64)
-        vgrp = keep.tile([P, 2, F, 4], BF16, name="vgrp", align_bytes=64)
-        qcodes = keep.tile([P, NQ], U32, name="qcodes", align_bytes=64)
-        kcodes = keep.tile([P, NK], U32, name="kcodes", align_bytes=64)
-        vcodes = keep.tile([P, 2 * F], U32, name="vcodes", align_bytes=64)
-        qscl = keep.tile([P, NQ], U8, name="qscl", align_bytes=64)
-        kscl = keep.tile([P, NK], U8, name="kscl", align_bytes=64)
-        vscl = keep.tile([P, 2 * F], U8, name="vscl", align_bytes=64)
-        m = [keep.tile([P, NK], F32, name="m%d" % i) for i in range(QT)]
-        e = [keep.tile([P, NK], BF16, name="e%d" % i) for i in range(QT)]
-        egrp = [keep.tile([P, 2, P, 4], BF16, name="egrp%d" % i, align_bytes=64) for i in range(QT)]
-        ecodes = [keep.tile([P, 2 * P], U32, name="ecodes%d" % i, align_bytes=64) for i in range(QT)]
-        escl = [keep.tile([P, 2 * P], U8, name="escl%d" % i, align_bytes=64) for i in range(QT)]
-        o_sb = [keep.tile([P, F], F32, name="o_sb%d" % i) for i in range(QT)]
-        nmax = [keep.tile([P, 1], F32, name="nmax%d" % i) for i in range(QT)]
-        esum = [keep.tile([P, 1], F32, name="esum%d" % i) for i in range(QT)]
-        rsum = [keep.tile([P, 1], F32, name="rsum%d" % i) for i in range(QT)]
-        ps = {}
+        def load_pair(raw, view, a):
+            nc.sync.dma_start(out=raw[a][:], in_=view[:, 2 * a:2 * a + 2, :])
 
-        def LQ(a):
-            nc.sync.dma_start(out=qraw[a][:], in_=q_view[:, 2 * a:2 * a + 2, :])
+        load_pair(q_raw, q_view, 0)
+        for a in range(PAIRS):
+            load_pair(k_raw, k_view, a)
+        load_pair(q_raw, q_view, 1)
+        load_pair(a_raw, a_view, 0)
+        load_pair(q_raw, q_view, 2)
+        load_pair(q_raw, q_view, 3)
+        load_pair(a_raw, a_view, 1)
+        for c in range(2):
+            nc.sync.dma_start(out=v_raw[c][:], in_=v_view[:, PACK * c:PACK * (c + 1), :])
+        load_pair(a_raw, a_view, 2)
+        load_pair(a_raw, a_view, 3)
 
-        def LK(a):
-            nc.sync.dma_start(out=kraw[a][:], in_=k_view[:, 2 * a:2 * a + 2, :])
-
-        def LA(a):
-            nc.sync.dma_start(out=araw[a][:], in_=a_view[:, 2 * a:2 * a + 2, :])
-
-        def LV(c):
-            nc.sync.dma_start(out=vraw[c][:], in_=v_view[:, 4 * c:4 * c + 4, :])
-
-        def copy_on(eng, dst, src):
-            if eng == "S":
+        def copy_out(engine, dst, src):
+            if engine == "scalar":
                 nc.scalar.copy(out=dst, in_=src)
             else:
                 nc.vector.tensor_copy(out=dst, in_=src)
 
-        def flip(key, raw, tag):
-            xt = pools[tag].tile([P, 2, 2, P], F32, tag=tag, name="xt_" + key)
+        def flip_pair(raw, grouped, a, engine):
+            planes = flip_banks.tile([P, 2, 2, P], F32, tag="flip", name="planes")
             for j in range(2):
-                words = raw[:, j, :].bitcast(F32)
+                words = raw[a][:, j, :].bitcast(F32)
                 for u in range(2):
-                    nc.tensor.transpose(xt[:, j, u, :], words[:, u * P:(u + 1) * P], ident_f[:])
-            ps[key] = xt
+                    nc.tensor.transpose(planes[:, j, u, :], words[:, u * P:(u + 1) * P], ident_f32[:])
+            dst = grouped[:, a * 2 * P * PACK:(a + 1) * 2 * P * PACK].bitcast(F32)
+            copy_out(engine, dst.rearrange("p (j r u) -> p j r u", j=2, u=2),
+                     planes[:].rearrange("p j u r -> p j r u"))
 
-        def unflip(key, grp, a, eng):
-            dst = grp[:, a * 1024:(a + 1) * 1024].bitcast(F32).rearrange(
-                "p (j r u) -> p j r u", j=2, u=2)
-            copy_on(eng, dst, ps[key][:].rearrange("p j u r -> p j r u"))
-
-        def quantise(grp, codes, scl, lo, hi):
+        def quantise(grouped, codes, scales, lo, hi):
             nc.vector.quantize_mx(
-                out=codes[:, lo:hi].bitcast(FP8X4), scales=scl[:, lo:hi], in_=grp[:, 4 * lo:4 * hi])
+                out=codes[:, lo:hi].bitcast(FP8X4), scales=scales[:, lo:hi],
+                in_=grouped[:, PACK * lo:PACK * hi])
 
-        def TQ(a, tag="o"):
-            flip("q%d" % a, qraw[a], tag)
+        def regroup_v(c):
+            nc.gpsimd.tensor_scalar(
+                out=v_grouped[:, c, :, :], in0=v_raw[c][:].rearrange("p t f -> p f t"),
+                scalar1=1.0, scalar2=0.0, op0=ALU.mult, op1=ALU.add)
 
-        def evQ(a, eng):
-            unflip("q%d" % a, qgrp, a, eng)
-
-        def qQ(a):
-            quantise(qgrp, qcodes, qscl, 256 * a, 256 * (a + 1))
-
-        def TK(a, tag="t"):
-            flip("k%d" % a, kraw[a], tag)
-
-        def evK(a, eng):
-            unflip("k%d" % a, kgrp, a, eng)
-
-        def qK(h):
-            quantise(kgrp, kcodes, kscl, 512 * h, 512 * (h + 1))
-
-        def VR(c, eng):
-            src = vraw[c][:].rearrange("p t f -> p f t")
-            if eng == "G":
-                nc.gpsimd.tensor_scalar(
-                    out=vgrp[:, c, :, :], in0=src, scalar1=1.0, scalar2=0.0,
-                    op0=ALU.mult, op1=ALU.add)
-            else:
-                copy_on(eng, vgrp[:, c, :, :], src)
-
-        def VQ(c):
+        def quantise_v(c):
             nc.vector.quantize_mx(
-                out=vcodes[:, c * F:(c + 1) * F].bitcast(FP8X4),
-                scales=vscl[:, c * F:(c + 1) * F],
-                in_=vgrp[:, c, :, :].rearrange("p f t -> p (f t)"))
+                out=v_codes[:, c * F:(c + 1) * F].bitcast(FP8X4), scales=v_scales[:, c * F:(c + 1) * F],
+                in_=v_grouped[:, c, :, :].rearrange("p f t -> p (f t)"))
 
-        def A_(i, h):
-            s = pools["s"].tile([P, 512], F32, tag="s", name="s%d_%d" % (i, h))
+        def scores(n):
+            if n >= 2 * QT:
+                return
+            i, h = divmod(n, 2)
+            bank = score_banks.tile([P, HALF], F32, tag="scores", name="bank")
             nc.tensor.matmul_mx(
-                out=s[:],
-                lhsT=qcodes[:, i * P:(i + 1) * P].bitcast(FP8X4),
-                lhsT_scale=qscl[:, i * P:(i + 1) * P],
-                rhs=kcodes[:, h * 512:(h + 1) * 512].bitcast(FP8X4),
-                rhs_scale=kscl[:, h * 512:(h + 1) * 512],
+                out=bank[:],
+                lhsT=q_codes[:, i * P:(i + 1) * P].bitcast(FP8X4),
+                lhsT_scale=q_scales[:, i * P:(i + 1) * P],
+                rhs=k_codes[:, h * HALF:(h + 1) * HALF].bitcast(FP8X4),
+                rhs_scale=k_scales[:, h * HALF:(h + 1) * HALF],
                 start=True, stop=True)
-            ps["s%d_%d" % (i, h)] = s
+            in_psum["scores", n] = bank
 
-        def M(i, h):
+        def mask_product(n):
+            i, h = divmod(n, 2)
             nc.vector.scalar_tensor_tensor(
-                out=m[i][:, h * 512:(h + 1) * 512],
-                in0=ps["s%d_%d" % (i, h)][:],
-                scalar=INV_SQRT_F,
-                in1=araw[i // 2][:, i % 2, h * 512:(h + 1) * 512],
+                out=masked[i][:, h * HALF:(h + 1) * HALF], in0=in_psum["scores", n][:],
+                scalar=INV_SQRT_F, in1=a_raw[i // 2][:, i % 2, h * HALF:(h + 1) * HALF],
                 op0=ALU.mult, op1=ALU.mult)
 
-        def X(i):
+        def negative_row_max(i):
             nc.vector.tensor_reduce(
-                out=nmax[i][:], in_=m[i][:], axis=mybir.AxisListType.X, op=ALU.max, negate=True)
+                out=neg_max[i][:], in_=masked[i][:], axis=mybir.AxisListType.X, op=ALU.max, negate=True)
 
-        def E(i):
+        def exponentials(i):
             nc.scalar.activation(
-                out=e[i][:], in_=m[i][:], func=ACT.Exp, bias=nmax[i][:], scale=1.0,
-                accum_out=esum[i][:])
+                out=e_rows[i][:], in_=masked[i][:], func=ACT.Exp, bias=neg_max[i][:], scale=1.0,
+                accum_out=e_sum[i][:])
 
-        def B(i, c):
-            et = pools["t"].tile([P, 4, P], BF16, tag="t", name="et%d_%d" % (i, c))
-            for t in range(4):
-                b = 4 * c + t
-                nc.tensor.transpose(et[:, t, :], e[i][:, b * P:(b + 1) * P], ident_b[:])
-            ps["et%d_%d" % (i, c)] = et
+        def transpose_e(i):
+            for c in range(2):
+                planes = flip_banks.tile([P, PACK, P], BF16, tag="flip", name="e_planes")
+                for t in range(PACK):
+                    b = PACK * c + t
+                    nc.tensor.transpose(planes[:, t, :], e_rows[i][:, b * P:(b + 1) * P], ident_bf16[:])
+                in_psum["e", i, c] = planes
 
-        def G(i, c, eng="S"):
-            copy_on(eng, egrp[i][:, c, :, :], ps["et%d_%d" % (i, c)][:].rearrange("p t r -> p r t"))
+        def regroup_e(i):
+            for c in range(2):
+                engine = "vector" if (c == 0 and i >= VECTOR_HELPS_FROM) else "scalar"
+                copy_out(engine, e_grouped[i][:, c, :, :], in_psum["e", i, c][:].rearrange("p t r -> p r t"))
 
-        def Qz(i):
+        def quantise_e(i):
             nc.vector.quantize_mx(
-                out=ecodes[i][:].bitcast(FP8X4), scales=escl[i][:],
-                in_=egrp[i][:].rearrange("p c r t -> p (c r t)"))
+                out=e_codes[i][:].bitcast(FP8X4), scales=e_scales[i][:],
+                in_=e_grouped[i][:].rearrange("p c r t -> p (c r t)"))
+            nc.vector.reciprocal(inv_sum[i][:], e_sum[i][:])
 
-        def R(i):
-            nc.vector.reciprocal(rsum[i][:], esum[i][:])
-
-        def C(i):
-            o_ps = pools["o"].tile([P, F], F32, tag="o", name="o_ps%d" % i)
+        def second_matmul(i):
+            bank = out_banks.tile([P, F], F32, tag="out", name="out_bank")
             for c in range(2):
                 nc.tensor.matmul_mx(
-                    out=o_ps[:],
-                    lhsT=ecodes[i][:, c * P:(c + 1) * P].bitcast(FP8X4),
-                    lhsT_scale=escl[i][:, c * P:(c + 1) * P],
-                    rhs=vcodes[:, c * F:(c + 1) * F].bitcast(FP8X4),
-                    rhs_scale=vscl[:, c * F:(c + 1) * F],
+                    out=bank[:],
+                    lhsT=e_codes[i][:, c * P:(c + 1) * P].bitcast(FP8X4),
+                    lhsT_scale=e_scales[i][:, c * P:(c + 1) * P],
+                    rhs=v_codes[:, c * F:(c + 1) * F].bitcast(FP8X4),
+                    rhs_scale=v_scales[:, c * F:(c + 1) * F],
                     start=(c == 0), stop=(c == 1))
-            ps["o%d" % i] = o_ps
+            in_psum["out", i] = bank
 
-        def O(i, eng="S"):
-            if eng == "S":
-                nc.scalar.activation(
-                    out=o_sb[i][:], in_=ps["o%d" % i][:], func=ACT.Copy, scale=rsum[i][:])
-            else:
-                nc.vector.tensor_scalar(
-                    out=o_sb[i][:], in0=ps["o%d" % i][:], scalar1=rsum[i][:], scalar2=None,
-                    op0=ALU.mult)
-            nc.sync.dma_start(out=o_view[:, i, :], in_=o_sb[i][:])
+        def output(i):
+            nc.scalar.activation(
+                out=result[i][:], in_=in_psum["out", i][:], func=ACT.Copy, scale=inv_sum[i][:])
+            nc.sync.dma_start(out=o_view[:, i, :], in_=result[i][:])
 
-        LQ(0)
-        LK(0)
-        LK(1)
-        LK(2)
-        LK(3)
-        LA(0)
-        LQ(1)
-        LQ(2)
-        LQ(3)
-        LA(1)
-        LV(0)
-        LV(1)
-        LA(2)
-        LA(3)
-        TQ(0)
-        evQ(0, "S")
-        qQ(0)
-        TK(0, "t")
-        evK(0, "V")
-        TK(1, "t")
-        evK(1, "S")
-        qK(0)
-        TK(2, "t")
-        evK(2, "V")
-        TK(3, "s")
-        evK(3, "S")
-        qK(1)
-        A_(0, 0)
-        A_(1, 0)
-        TQ(1)
-        evQ(1, "S")
-        TQ(2)
-        evQ(2, "S")
-        A_(0, 1)
-        VR(0, "G")
-        VR(1, "G")
-        M(0, 0)
-        A_(1, 1)
-        TQ(3)
-        evQ(3, "S")
-        M(1, 0)
-        M(0, 1)
-        X(0)
-        qQ(1)
-        A_(2, 0)
-        A_(2, 1)
-        M(1, 1)
-        A_(3, 0)
-        E(0)
-        B(0, 0)
-        B(0, 1)
-        X(1)
-        qQ(2)
-        E(1)
-        G(0, 0)
-        G(0, 1)
-        B(1, 0)
-        B(1, 1)
-        M(2, 0)
-        A_(3, 1)
-        M(2, 1)
-        A_(4, 0)
-        X(2)
-        qQ(3)
-        E(2)
-        G(1, 0)
-        G(1, 1)
-        B(2, 0)
-        B(2, 1)
-        M(3, 0)
-        A_(4, 1)
-        M(3, 1)
-        A_(5, 0)
-        X(3)
-        E(3)
-        G(2, 0)
-        G(2, 1)
-        B(3, 0)
-        B(3, 1)
-        M(4, 0)
-        A_(5, 1)
-        M(4, 1)
-        A_(6, 0)
-        X(4)
-        VQ(0)
-        VQ(1)
-        Qz(0)
-        R(0)
-        C(0)
-        E(4)
-        G(3, 0)
-        G(3, 1)
-        B(4, 0)
-        B(4, 1)
-        O(0, "S")
-        M(5, 0)
-        A_(6, 1)
-        M(5, 1)
-        A_(7, 0)
-        X(5)
-        Qz(1)
-        R(1)
-        C(1)
-        E(5)
-        G(4, 0)
-        G(4, 1)
-        B(5, 0)
-        B(5, 1)
-        O(1, "S")
-        M(6, 0)
-        A_(7, 1)
-        M(6, 1)
-        X(6)
-        Qz(2)
-        R(2)
-        C(2)
-        E(6)
-        G(5, 0)
-        G(5, 1)
-        B(6, 0)
-        B(6, 1)
-        O(2, "S")
-        M(7, 0)
-        M(7, 1)
-        X(7)
-        Qz(3)
-        Qz(4)
-        E(7)
-        C(3)
-        R(3)
-        G(6, 0, "V")
-        Qz(5)
-        C(4)
-        G(6, 1, "V")
-        O(3, "S")
-        B(7, 0)
-        R(4)
-        Qz(6)
-        B(7, 1)
-        O(4, "S")
-        C(5)
-        R(5)
-        G(7, 0, "V")
-        G(7, 1, "S")
-        C(6)
-        R(6)
-        R(7)
-        Qz(7)
-        O(5, "S")
-        O(6, "V")
-        C(7)
-        O(7, "S")
+        flip_pair(q_raw, q_grouped, 0, "scalar")
+        quantise(q_grouped, q_codes, q_scales, 0, 2 * P)
+        for a in range(PAIRS):
+            flip_pair(k_raw, k_grouped, a, "scalar" if a % 2 else "vector")
+            if a % 2:
+                quantise(k_grouped, k_codes, k_scales, (a - 1) * 2 * P, (a + 1) * 2 * P)
+        flip_pair(q_raw, q_grouped, 1, "scalar")
+        for n in range(SCORES_AHEAD):
+            scores(n)
+        for a in range(2, PAIRS):
+            flip_pair(q_raw, q_grouped, a, "scalar")
+        for c in range(2):
+            regroup_v(c)
+
+        for s in range(QT + SECOND_STAGE_LAG):
+            late = s - SECOND_STAGE_LAG
+            if s < QT:
+                mask_product(2 * s)
+                if s % 2 == 0 and s // 2 + 1 < PAIRS:
+                    a = s // 2 + 1
+                    quantise(q_grouped, q_codes, q_scales, a * 2 * P, (a + 1) * 2 * P)
+                scores(2 * s + SCORES_AHEAD)
+                mask_product(2 * s + 1)
+                scores(2 * s + 1 + SCORES_AHEAD)
+                negative_row_max(s)
+            if late == 0:
+                for c in range(2):
+                    quantise_v(c)
+            if late >= 0:
+                quantise_e(late)
+                second_matmul(late)
+            if s < QT:
+                exponentials(s)
+            if 1 <= s <= QT:
+                regroup_e(s - 1)
+            if s < QT:
+                transpose_e(s)
+            if late >= 0:
+                output(late)

@@ -26,6 +26,7 @@ INV_SQRT_F = 1.0 / math.sqrt(F)
 SCORES_AHEAD = 3
 SECOND_STAGE_LAG = 3
 VECTOR_HELPS_FROM = QT - 2
+Q_PAIR_BEHIND_MASK = {0: 1, 2: 2, 3: 3}
 
 
 def tile_attention_prop_pb_kernel(tc, A, qe1, ke1, ve1, out):
@@ -41,6 +42,10 @@ def tile_attention_prop_pb_kernel(tc, A, qe1, ke1, ve1, out):
         make_identity(nc, ident_f32[:])
         ident_bf16 = sbuf.tile([P, P], BF16, name="ident_bf16")
         make_identity(nc, ident_bf16[:])
+
+        warm = sbuf.tile([P, 1], F32, name="warm")
+        nc.vector.memset(warm[:], 0.0)
+        nc.scalar.activation(out=warm[:], in_=warm[:], func=ACT.Exp)
 
         q_raw = [sbuf.tile([P, 2, F], BF16, name="q_raw%d" % a) for a in range(PAIRS)]
         k_raw = [sbuf.tile([P, 2, F], BF16, name="k_raw%d" % a) for a in range(PAIRS)]
@@ -84,9 +89,9 @@ def tile_attention_prop_pb_kernel(tc, A, qe1, ke1, ve1, out):
         load_pair(q_raw, q_view, 2)
         load_pair(q_raw, q_view, 3)
         load_pair(a_raw, a_view, 1)
+        load_pair(a_raw, a_view, 2)
         for c in range(2):
             nc.sync.dma_start(out=v_raw[c][:], in_=v_view[:, PACK * c:PACK * (c + 1), :])
-        load_pair(a_raw, a_view, 2)
         load_pair(a_raw, a_view, 3)
 
         def copy_out(engine, dst, src):
@@ -203,13 +208,12 @@ def tile_attention_prop_pb_kernel(tc, A, qe1, ke1, ve1, out):
         for s in range(QT + SECOND_STAGE_LAG):
             late = s - SECOND_STAGE_LAG
             if s < QT:
-                mask_product(2 * s)
-                if s % 2 == 0 and s // 2 + 1 < PAIRS:
-                    a = s // 2 + 1
-                    quantise(q_grouped, q_codes, q_scales, a * 2 * P, (a + 1) * 2 * P)
-                scores(2 * s + SCORES_AHEAD)
-                mask_product(2 * s + 1)
-                scores(2 * s + 1 + SCORES_AHEAD)
+                for n in (2 * s, 2 * s + 1):
+                    mask_product(n)
+                    if n in Q_PAIR_BEHIND_MASK:
+                        a = Q_PAIR_BEHIND_MASK[n]
+                        quantise(q_grouped, q_codes, q_scales, a * 2 * P, (a + 1) * 2 * P)
+                    scores(n + SCORES_AHEAD)
                 negative_row_max(s)
             if late == 0:
                 for c in range(2):

@@ -24,9 +24,8 @@ FLOPS = 2 * NQ * NK * F * 2
 INV_SQRT_F = 1.0 / math.sqrt(F)
 
 SCORES_AHEAD = 3
-SECOND_STAGE_LAG = 3
-VECTOR_HELPS_FROM = QT - 2
-Q_PAIR_BEHIND_MASK = {0: 1, 2: 2, 3: 3}
+SECOND_STAGE_LAG = 4
+OUT_BANKS = 2
 
 
 def tile_attention_prop_pb_kernel(tc, A, qe1, ke1, ve1, out):
@@ -35,17 +34,13 @@ def tile_attention_prop_pb_kernel(tc, A, qe1, ke1, ve1, out):
         sbuf = ctx.enter_context(tc.tile_pool(name="sbuf", bufs=1))
         score_banks = ctx.enter_context(tc.psum_pool(name="score_banks", bufs=SCORES_AHEAD))
         flip_banks = ctx.enter_context(tc.psum_pool(name="flip_banks", bufs=3))
-        out_banks = ctx.enter_context(tc.psum_pool(name="out_banks", bufs=2))
+        out_banks = ctx.enter_context(tc.psum_pool(name="out_banks", bufs=OUT_BANKS))
         ctx.enter_context(tc.manual_schedule())
 
         ident_f32 = sbuf.tile([P, P], F32, name="ident_f32")
         make_identity(nc, ident_f32[:])
         ident_bf16 = sbuf.tile([P, P], BF16, name="ident_bf16")
         make_identity(nc, ident_bf16[:])
-
-        warm = sbuf.tile([P, 1], F32, name="warm")
-        nc.vector.memset(warm[:], 0.0)
-        nc.scalar.activation(out=warm[:], in_=warm[:], func=ACT.Exp)
 
         q_raw = [sbuf.tile([P, 2, F], BF16, name="q_raw%d" % a) for a in range(PAIRS)]
         k_raw = [sbuf.tile([P, 2, F], BF16, name="k_raw%d" % a) for a in range(PAIRS)]
@@ -89,9 +84,9 @@ def tile_attention_prop_pb_kernel(tc, A, qe1, ke1, ve1, out):
         load_pair(q_raw, q_view, 2)
         load_pair(q_raw, q_view, 3)
         load_pair(a_raw, a_view, 1)
-        load_pair(a_raw, a_view, 2)
         for c in range(2):
             nc.sync.dma_start(out=v_raw[c][:], in_=v_view[:, PACK * c:PACK * (c + 1), :])
+        load_pair(a_raw, a_view, 2)
         load_pair(a_raw, a_view, 3)
 
         def copy_out(engine, dst, src):
@@ -163,16 +158,20 @@ def tile_attention_prop_pb_kernel(tc, A, qe1, ke1, ve1, out):
                     nc.tensor.transpose(planes[:, t, :], e_rows[i][:, b * P:(b + 1) * P], ident_bf16[:])
                 in_psum["e", i, c] = planes
 
-        def regroup_e(i):
+        def regroup_e(i, engines):
             for c in range(2):
-                engine = "vector" if (c == 0 and i >= VECTOR_HELPS_FROM) else "scalar"
-                copy_out(engine, e_grouped[i][:, c, :, :], in_psum["e", i, c][:].rearrange("p t r -> p r t"))
+                copy_out(engines[c], e_grouped[i][:, c, :, :],
+                         in_psum["e", i, c][:].rearrange("p t r -> p r t"))
 
         def quantise_e(i):
             nc.vector.quantize_mx(
                 out=e_codes[i][:].bitcast(FP8X4), scales=e_scales[i][:],
                 in_=e_grouped[i][:].rearrange("p c r t -> p (c r t)"))
             nc.vector.reciprocal(inv_sum[i][:], e_sum[i][:])
+
+        def second_stage(i):
+            quantise_e(i)
+            second_matmul(i)
 
         def second_matmul(i):
             bank = out_banks.tile([P, F], F32, tag="out", name="out_bank")
@@ -186,10 +185,24 @@ def tile_attention_prop_pb_kernel(tc, A, qe1, ke1, ve1, out):
                     start=(c == 0), stop=(c == 1))
             in_psum["out", i] = bank
 
-        def output(i):
-            nc.scalar.activation(
-                out=result[i][:], in_=in_psum["out", i][:], func=ACT.Copy, scale=inv_sum[i][:])
+        def output(i, engine):
+            if engine == "scalar":
+                nc.scalar.activation(
+                    out=result[i][:], in_=in_psum["out", i][:], func=ACT.Copy, scale=inv_sum[i][:])
+            else:
+                nc.vector.tensor_scalar(
+                    out=result[i][:], in0=in_psum["out", i][:], scalar1=inv_sum[i][:], scalar2=None,
+                    op0=ALU.mult)
             nc.sync.dma_start(out=o_view[:, i, :], in_=result[i][:])
+
+        def mask_and_max(s):
+            for n in (2 * s, 2 * s + 1):
+                mask_product(n)
+                if n % 4 == 0 and n // 4 + 1 < PAIRS:
+                    a = n // 4 + 1
+                    quantise(q_grouped, q_codes, q_scales, a * 2 * P, (a + 1) * 2 * P)
+                scores(n + SCORES_AHEAD)
+            negative_row_max(s)
 
         flip_pair(q_raw, q_grouped, 0, "scalar")
         quantise(q_grouped, q_codes, q_scales, 0, 2 * P)
@@ -205,27 +218,36 @@ def tile_attention_prop_pb_kernel(tc, A, qe1, ke1, ve1, out):
         for c in range(2):
             regroup_v(c)
 
-        for s in range(QT + SECOND_STAGE_LAG):
+        last = QT - 1
+        for s in range(last):
             late = s - SECOND_STAGE_LAG
-            if s < QT:
-                for n in (2 * s, 2 * s + 1):
-                    mask_product(n)
-                    if n in Q_PAIR_BEHIND_MASK:
-                        a = Q_PAIR_BEHIND_MASK[n]
-                        quantise(q_grouped, q_codes, q_scales, a * 2 * P, (a + 1) * 2 * P)
-                    scores(n + SCORES_AHEAD)
-                negative_row_max(s)
+            mask_and_max(s)
             if late == 0:
                 for c in range(2):
                     quantise_v(c)
             if late >= 0:
-                quantise_e(late)
-                second_matmul(late)
-            if s < QT:
-                exponentials(s)
-            if 1 <= s <= QT:
-                regroup_e(s - 1)
-            if s < QT:
-                transpose_e(s)
+                second_stage(late)
+            exponentials(s)
+            if s >= 1:
+                regroup_e(s - 1, ("scalar", "scalar"))
+            transpose_e(s)
             if late >= 0:
-                output(late)
+                output(late, "scalar")
+
+        left = list(range(last - SECOND_STAGE_LAG, last))
+        mask_and_max(last)
+        for j in left[:OUT_BANKS]:
+            second_stage(j)
+        exponentials(last)
+        regroup_e(last - 1, ("vector", "vector"))
+        for j in left[:OUT_BANKS]:
+            output(j, "scalar")
+        transpose_e(last)
+        for j in left[OUT_BANKS:]:
+            second_stage(j)
+        regroup_e(last, ("vector", "scalar"))
+        quantise_e(last)
+        for j, engine in zip(left[OUT_BANKS:], ("scalar", "vector")):
+            output(j, engine)
+        second_matmul(last)
+        output(last, "scalar")

@@ -79,10 +79,9 @@ def tile_attention_prop_pb_kernel(tc, A, qe1, ke1, ve1, out):
         load_pair(q_raw, q_view, 0)
         for a in range(PAIRS):
             load_pair(k_raw, k_view, a)
-        load_pair(q_raw, q_view, 1)
         load_pair(a_raw, a_view, 0)
-        load_pair(q_raw, q_view, 2)
-        load_pair(q_raw, q_view, 3)
+        for a in range(1, PAIRS):
+            load_pair(q_raw, q_view, a)
         load_pair(a_raw, a_view, 1)
         for c in range(2):
             nc.sync.dma_start(out=v_raw[c][:], in_=v_view[:, PACK * c:PACK * (c + 1), :])
@@ -95,8 +94,8 @@ def tile_attention_prop_pb_kernel(tc, A, qe1, ke1, ve1, out):
             else:
                 nc.vector.tensor_copy(out=dst, in_=src)
 
-        def flip_pair(raw, grouped, a, engine):
-            planes = flip_banks.tile([P, 2, 2, P], F32, tag="flip", name="planes")
+        def flip_pair(raw, grouped, a, banks, tag, engine):
+            planes = banks.tile([P, 2, 2, P], F32, tag=tag, name="planes")
             for j in range(2):
                 words = raw[a][:, j, :].bitcast(F32)
                 for u in range(2):
@@ -195,33 +194,46 @@ def tile_attention_prop_pb_kernel(tc, A, qe1, ke1, ve1, out):
                     op0=ALU.mult)
             nc.sync.dma_start(out=o_view[:, i, :], in_=result[i][:])
 
-        def mask_and_max(s):
-            for n in (2 * s, 2 * s + 1):
-                mask_product(n)
-                if n % 4 == 0 and n // 4 + 1 < PAIRS:
-                    a = n // 4 + 1
-                    quantise(q_grouped, q_codes, q_scales, a * 2 * P, (a + 1) * 2 * P)
-                scores(n + SCORES_AHEAD)
-            negative_row_max(s)
+        def flip_q(a):
+            flip_pair(q_raw, q_grouped, a, out_banks, "out", "scalar")
 
-        flip_pair(q_raw, q_grouped, 0, "scalar")
-        quantise(q_grouped, q_codes, q_scales, 0, 2 * P)
+        def quantise_q(a):
+            quantise(q_grouped, q_codes, q_scales, a * 2 * P, (a + 1) * 2 * P)
+
+        flip_q(0)
+        quantise_q(0)
         for a in range(PAIRS):
-            flip_pair(k_raw, k_grouped, a, "scalar" if a % 2 else "vector")
+            flip_pair(k_raw, k_grouped, a, flip_banks, "flip", "scalar" if a % 2 else "vector")
             if a % 2:
                 quantise(k_grouped, k_codes, k_scales, (a - 1) * 2 * P, (a + 1) * 2 * P)
-        flip_pair(q_raw, q_grouped, 1, "scalar")
-        for n in range(SCORES_AHEAD):
-            scores(n)
-        for a in range(2, PAIRS):
-            flip_pair(q_raw, q_grouped, a, "scalar")
+        scores(0)
+        scores(2)
+        flip_q(1)
+        flip_q(2)
+        scores(1)
         for c in range(2):
             regroup_v(c)
+        mask_product(0)
+        scores(3)
+        flip_q(3)
+        mask_product(2)
+        mask_product(1)
 
         last = QT - 1
         for s in range(last):
             late = s - SECOND_STAGE_LAG
-            mask_and_max(s)
+            if s >= 2:
+                for n in (2 * s, 2 * s + 1):
+                    mask_product(n)
+                    scores(n + SCORES_AHEAD)
+            negative_row_max(s)
+            if s + 1 < PAIRS:
+                quantise_q(s + 1)
+            if s == 0:
+                scores(4)
+                scores(5)
+                mask_product(3)
+                scores(6)
             if late == 0:
                 for c in range(2):
                     quantise_v(c)
@@ -235,7 +247,9 @@ def tile_attention_prop_pb_kernel(tc, A, qe1, ke1, ve1, out):
                 output(late, "scalar")
 
         left = list(range(last - SECOND_STAGE_LAG, last))
-        mask_and_max(last)
+        mask_product(2 * last)
+        mask_product(2 * last + 1)
+        negative_row_max(last)
         for j in left[:OUT_BANKS]:
             second_stage(j)
         exponentials(last)

@@ -203,19 +203,17 @@ def tile_attention_prop_pb_kernel(tc, A, qe1, ke1, ve1, out):
         flip_q(0)
         quantise_q(0)
         for a in range(PAIRS):
-            flip_pair(k_raw, k_grouped, a, flip_banks, "flip", "scalar" if a % 2 else "vector")
-            if a % 2:
-                quantise(k_grouped, k_codes, k_scales, (a - 1) * 2 * P, (a + 1) * 2 * P)
+            flip_pair(k_raw, k_grouped, a, flip_banks, "flip", "scalar")
+            quantise(k_grouped, k_codes, k_scales, a * 2 * P, (a + 1) * 2 * P)
         scores(0)
         scores(2)
-        flip_q(1)
-        flip_q(2)
         scores(1)
         for c in range(2):
             regroup_v(c)
         mask_product(0)
         scores(3)
-        flip_q(3)
+        for a in range(1, PAIRS):
+            flip_q(a)
         mask_product(2)
         mask_product(1)
 

@@ -39,13 +39,11 @@ def tile_attention_prop_pb_kernel(tc, A, qe1, ke1, ve1, out):
 
         ident_f32 = sbuf.tile([P, P], F32, name="ident_f32")
         make_identity(nc, ident_f32[:])
-        ident_bf16 = sbuf.tile([P, P], BF16, name="ident_bf16")
-        make_identity(nc, ident_bf16[:])
 
         q_raw = [sbuf.tile([P, 2, F], BF16, name="q_raw%d" % a) for a in range(PAIRS)]
         k_raw = [sbuf.tile([P, 2, F], BF16, name="k_raw%d" % a) for a in range(PAIRS)]
         a_raw = [sbuf.tile([P, 2, NK], BF16, name="a_raw%d" % a) for a in range(PAIRS)]
-        v_raw = [sbuf.tile([P, PACK, F], BF16, name="v_raw%d" % c) for c in range(2)]
+        v_raw = [sbuf.tile([P, 2, 2, F], BF16, name="v_raw%d" % c) for c in range(2)]
         q_grouped = sbuf.tile([P, NQ * PACK], BF16, name="q_grouped", align_bytes=64)
         k_grouped = sbuf.tile([P, NK * PACK], BF16, name="k_grouped", align_bytes=64)
         v_grouped = sbuf.tile([P, 2, F, PACK], BF16, name="v_grouped", align_bytes=64)
@@ -58,19 +56,19 @@ def tile_attention_prop_pb_kernel(tc, A, qe1, ke1, ve1, out):
         masked = [sbuf.tile([P, NK], F32, name="masked%d" % i) for i in range(QT)]
         neg_max = [sbuf.tile([P, 1], F32, name="neg_max%d" % i) for i in range(QT)]
         e_rows = [sbuf.tile([P, NK], BF16, name="e_rows%d" % i) for i in range(QT)]
-        e_sum = [sbuf.tile([P, 1], F32, name="e_sum%d" % i) for i in range(QT)]
+        e_sum = sbuf.tile([P, QT], F32, name="e_sum")
         e_grouped = [
             sbuf.tile([P, 2, P, PACK], BF16, name="e_grouped%d" % i, align_bytes=64) for i in range(QT)]
         e_codes = [sbuf.tile([P, 2 * P], U32, name="e_codes%d" % i, align_bytes=64) for i in range(QT)]
         e_scales = [sbuf.tile([P, 2 * P], U8, name="e_scales%d" % i, align_bytes=64) for i in range(QT)]
-        inv_sum = [sbuf.tile([P, 1], F32, name="inv_sum%d" % i) for i in range(QT)]
+        inv_sum = [sbuf.tile([P, QT // 2], F32, name="inv_sum%d" % g) for g in range(2)]
         result = [sbuf.tile([P, F], F32, name="result%d" % i) for i in range(QT)]
         in_psum = {}
 
         q_view = qe1.rearrange("(p i) f -> p i f", i=QT)
         k_view = ke1.rearrange("(j p) f -> p j f", p=P)
         a_view = A.rearrange("(p i) k -> p i k", i=QT)
-        v_view = ve1.rearrange("(b p) f -> p b f", p=P)
+        v_view = ve1.rearrange("(b p e) f -> p b e f", p=P, e=2)
         o_view = out.rearrange("(p i) f -> p i f", i=QT)
 
         def load_pair(raw, view, a):
@@ -84,7 +82,7 @@ def tile_attention_prop_pb_kernel(tc, A, qe1, ke1, ve1, out):
             load_pair(q_raw, q_view, a)
         load_pair(a_raw, a_view, 1)
         for c in range(2):
-            nc.sync.dma_start(out=v_raw[c][:], in_=v_view[:, PACK * c:PACK * (c + 1), :])
+            nc.sync.dma_start(out=v_raw[c][:], in_=v_view[:, 2 * c:2 * (c + 1), :, :])
         load_pair(a_raw, a_view, 2)
         load_pair(a_raw, a_view, 3)
 
@@ -111,7 +109,7 @@ def tile_attention_prop_pb_kernel(tc, A, qe1, ke1, ve1, out):
 
         def regroup_v(c):
             nc.gpsimd.tensor_scalar(
-                out=v_grouped[:, c, :, :], in0=v_raw[c][:].rearrange("p t f -> p f t"),
+                out=v_grouped[:, c, :, :], in0=v_raw[c][:].rearrange("p u e f -> p f (u e)"),
                 scalar1=1.0, scalar2=0.0, op0=ALU.mult, op1=ALU.add)
 
         def quantise_v(c):
@@ -147,26 +145,33 @@ def tile_attention_prop_pb_kernel(tc, A, qe1, ke1, ve1, out):
         def exponentials(i):
             nc.scalar.activation(
                 out=e_rows[i][:], in_=masked[i][:], func=ACT.Exp, bias=neg_max[i][:], scale=1.0,
-                accum_out=e_sum[i][:])
+                accum_out=e_sum[:, i:i + 1])
 
-        def transpose_e(i):
-            for c in range(2):
-                planes = flip_banks.tile([P, PACK, P], BF16, tag="flip", name="e_planes")
-                for t in range(PACK):
-                    b = PACK * c + t
-                    nc.tensor.transpose(planes[:, t, :], e_rows[i][:, b * P:(b + 1) * P], ident_bf16[:])
-                in_psum["e", i, c] = planes
+        def transpose_e(i, banks):
+            words = e_rows[i][:].bitcast(F32)
+            share = 2 // banks
+            for g in range(banks):
+                planes = flip_banks.tile([P, share, 2, P], F32, tag="flip", name="e_planes")
+                for j in range(share):
+                    for u in range(2):
+                        b = 2 * (g * share + j) + u
+                        nc.tensor.transpose(planes[:, j, u, :], words[:, b * P:(b + 1) * P], ident_f32[:])
+                in_psum["e", i, g] = planes
 
         def regroup_e(i, engines):
-            for c in range(2):
-                copy_out(engines[c], e_grouped[i][:, c, :, :],
-                         in_psum["e", i, c][:].rearrange("p t r -> p r t"))
+            share = 2 // len(engines)
+            for g, engine in enumerate(engines):
+                dst = e_grouped[i][:, g * share:(g + 1) * share, :, :].rearrange("p c r t -> p (c r t)").bitcast(F32)
+                copy_out(engine, dst.rearrange("p (c r u) -> p c r u", c=share, u=2),
+                         in_psum["e", i, g][:].rearrange("p c u r -> p c r u"))
 
         def quantise_e(i):
             nc.vector.quantize_mx(
                 out=e_codes[i][:].bitcast(FP8X4), scales=e_scales[i][:],
                 in_=e_grouped[i][:].rearrange("p c r t -> p (c r t)"))
-            nc.vector.reciprocal(inv_sum[i][:], e_sum[i][:])
+
+        def reciprocals(g):
+            nc.vector.reciprocal(inv_sum[g][:], e_sum[:, g * (QT // 2):(g + 1) * (QT // 2)])
 
         def second_stage(i):
             quantise_e(i)
@@ -185,12 +190,14 @@ def tile_attention_prop_pb_kernel(tc, A, qe1, ke1, ve1, out):
             in_psum["out", i] = bank
 
         def output(i, engine):
+            g, j = divmod(i, QT // 2)
+            inv = inv_sum[g][:, j:j + 1]
             if engine == "scalar":
                 nc.scalar.activation(
-                    out=result[i][:], in_=in_psum["out", i][:], func=ACT.Copy, scale=inv_sum[i][:])
+                    out=result[i][:], in_=in_psum["out", i][:], func=ACT.Copy, scale=inv)
             else:
                 nc.vector.tensor_scalar(
-                    out=result[i][:], in0=in_psum["out", i][:], scalar1=inv_sum[i][:], scalar2=None,
+                    out=result[i][:], in0=in_psum["out", i][:], scalar1=inv, scalar2=None,
                     op0=ALU.mult)
             nc.sync.dma_start(out=o_view[:, i, :], in_=result[i][:])
 
@@ -224,37 +231,41 @@ def tile_attention_prop_pb_kernel(tc, A, qe1, ke1, ve1, out):
                 for n in (2 * s, 2 * s + 1):
                     mask_product(n)
                     scores(n + SCORES_AHEAD)
-            negative_row_max(s)
             if s + 1 < PAIRS:
                 quantise_q(s + 1)
+            if late == 0:
+                for c in range(2):
+                    quantise_v(c)
+            if late >= 0:
+                second_stage(late)
+            negative_row_max(s)
             if s == 0:
                 scores(4)
                 scores(5)
                 mask_product(3)
                 scores(6)
             if late == 0:
-                for c in range(2):
-                    quantise_v(c)
-            if late >= 0:
-                second_stage(late)
+                reciprocals(0)
             exponentials(s)
             if s >= 1:
-                regroup_e(s - 1, ("scalar", "scalar"))
-            transpose_e(s)
+                regroup_e(s - 1, ("scalar",))
+            transpose_e(s, 1)
             if late >= 0:
                 output(late, "scalar")
 
         left = list(range(last - SECOND_STAGE_LAG, last))
         mask_product(2 * last)
         mask_product(2 * last + 1)
+        second_stage(left[0])
         negative_row_max(last)
-        for j in left[:OUT_BANKS]:
+        for j in left[1:OUT_BANKS]:
             second_stage(j)
         exponentials(last)
-        regroup_e(last - 1, ("vector", "vector"))
-        for j in left[:OUT_BANKS]:
-            output(j, "scalar")
-        transpose_e(last)
+        regroup_e(last - 1, ("vector",))
+        output(left[0], "scalar")
+        reciprocals(1)
+        output(left[1], "scalar")
+        transpose_e(last, 2)
         for j in left[OUT_BANKS:]:
             second_stage(j)
         regroup_e(last, ("vector", "scalar"))

@@ -24,6 +24,7 @@ FLOPS = 2 * NQ * NK * F * 2
 INV_SQRT_F = 1.0 / math.sqrt(F)
 
 SCORES_AHEAD = 3
+V_PIECE = 64
 SECOND_STAGE_LAG = 4
 OUT_BANKS = 2
 
@@ -108,9 +109,11 @@ def tile_attention_prop_pb_kernel(tc, A, qe1, ke1, ve1, out):
                 in_=grouped[:, PACK * lo:PACK * hi])
 
         def regroup_v(c):
-            nc.gpsimd.tensor_scalar(
-                out=v_grouped[:, c, :, :], in0=v_raw[c][:].rearrange("p u e f -> p f (u e)"),
-                scalar1=1.0, scalar2=0.0, op0=ALU.mult, op1=ALU.add)
+            for f in range(0, F, V_PIECE):
+                nc.gpsimd.tensor_scalar(
+                    out=v_grouped[:, c, f:f + V_PIECE, :],
+                    in0=v_raw[c][:, :, :, f:f + V_PIECE].rearrange("p u e f -> p f (u e)"),
+                    scalar1=1.0, scalar2=0.0, op0=ALU.mult, op1=ALU.add)
 
         def quantise_v(c):
             nc.vector.quantize_mx(

@@ -23,8 +23,10 @@ PAIRS = 4
 FLOPS = 2 * NQ * NK * F * 2
 INV_SQRT_F = 1.0 / math.sqrt(F)
 
-SCORES_AHEAD = 3
-V_PIECE = 64
+SCORES_AHEAD = 4
+LIFTED = (3,)
+MASK_PIECE = 512
+V_PIECE = 128
 SECOND_STAGE_LAG = 4
 OUT_BANKS = 2
 
@@ -34,16 +36,16 @@ def tile_attention_prop_pb_kernel(tc, A, qe1, ke1, ve1, out):
     with ExitStack() as ctx:
         sbuf = ctx.enter_context(tc.tile_pool(name="sbuf", bufs=1))
         score_banks = ctx.enter_context(tc.psum_pool(name="score_banks", bufs=SCORES_AHEAD))
-        flip_banks = ctx.enter_context(tc.psum_pool(name="flip_banks", bufs=3))
+        flip_banks = ctx.enter_context(tc.psum_pool(name="flip_banks", bufs=2))
         out_banks = ctx.enter_context(tc.psum_pool(name="out_banks", bufs=OUT_BANKS))
         ctx.enter_context(tc.manual_schedule())
 
         ident_f32 = sbuf.tile([P, P], F32, name="ident_f32")
         make_identity(nc, ident_f32[:])
 
-        q_raw = [sbuf.tile([P, 2, F], BF16, name="q_raw%d" % a) for a in range(PAIRS)]
-        k_raw = [sbuf.tile([P, 2, F], BF16, name="k_raw%d" % a) for a in range(PAIRS)]
-        a_raw = [sbuf.tile([P, 2, NK], BF16, name="a_raw%d" % a) for a in range(PAIRS)]
+        q_raw = sbuf.tile([P, QT, F], BF16, name="q_raw")
+        k_raw = sbuf.tile([P, PAIRS, 2, F], BF16, name="k_raw")
+        a_raw = sbuf.tile([P, QT, NK], BF16, name="a_raw")
         v_raw = [sbuf.tile([P, 2, 2, F], BF16, name="v_raw%d" % c) for c in range(2)]
         q_grouped = sbuf.tile([P, NQ * PACK], BF16, name="q_grouped", align_bytes=64)
         k_grouped = sbuf.tile([P, NK * PACK], BF16, name="k_grouped", align_bytes=64)
@@ -55,6 +57,7 @@ def tile_attention_prop_pb_kernel(tc, A, qe1, ke1, ve1, out):
         k_scales = sbuf.tile([P, NK], U8, name="k_scales", align_bytes=64)
         v_scales = sbuf.tile([P, 2 * F], U8, name="v_scales", align_bytes=64)
         masked = [sbuf.tile([P, NK], F32, name="masked%d" % i) for i in range(QT)]
+        lifted = {n: sbuf.tile([P, HALF], F32, name="lifted%d" % n) for n in LIFTED}
         neg_max = [sbuf.tile([P, 1], F32, name="neg_max%d" % i) for i in range(QT)]
         e_rows = [sbuf.tile([P, NK], BF16, name="e_rows%d" % i) for i in range(QT)]
         e_sum = sbuf.tile([P, QT], F32, name="e_sum")
@@ -62,30 +65,33 @@ def tile_attention_prop_pb_kernel(tc, A, qe1, ke1, ve1, out):
             sbuf.tile([P, 2, P, PACK], BF16, name="e_grouped%d" % i, align_bytes=64) for i in range(QT)]
         e_codes = [sbuf.tile([P, 2 * P], U32, name="e_codes%d" % i, align_bytes=64) for i in range(QT)]
         e_scales = [sbuf.tile([P, 2 * P], U8, name="e_scales%d" % i, align_bytes=64) for i in range(QT)]
+        half_sum = sbuf.tile([P, 2], F32, name="half_sum")
         inv_sum = [sbuf.tile([P, QT // 2], F32, name="inv_sum%d" % g) for g in range(2)]
         result = [sbuf.tile([P, F], F32, name="result%d" % i) for i in range(QT)]
         in_psum = {}
 
         q_view = qe1.rearrange("(p i) f -> p i f", i=QT)
-        k_view = ke1.rearrange("(j p) f -> p j f", p=P)
+        k_view = ke1.rearrange("(a p i) f -> p a i f", p=P, i=2)
         a_view = A.rearrange("(p i) k -> p i k", i=QT)
         v_view = ve1.rearrange("(b p e) f -> p b e f", p=P, e=2)
         o_view = out.rearrange("(p i) f -> p i f", i=QT)
 
-        def load_pair(raw, view, a):
-            nc.sync.dma_start(out=raw[a][:], in_=view[:, 2 * a:2 * a + 2, :])
+        def load(raw, view, lo, hi):
+            nc.sync.dma_start(out=raw[:, lo:hi], in_=view[:, lo:hi])
 
-        load_pair(q_raw, q_view, 0)
+        load(q_raw, q_view, 0, 1)
         for a in range(PAIRS):
-            load_pair(k_raw, k_view, a)
-        load_pair(a_raw, a_view, 0)
-        for a in range(1, PAIRS):
-            load_pair(q_raw, q_view, a)
-        load_pair(a_raw, a_view, 1)
+            load(k_raw, k_view, a, a + 1)
+        load(a_raw, a_view, 0, 1)
+        load(q_raw, q_view, 1, 2)
+        load(q_raw, q_view, 2, 4)
+        load(a_raw, a_view, 1, 2)
+        load(q_raw, q_view, 4, 8)
+        load(a_raw, a_view, 2, 4)
         for c in range(2):
             nc.sync.dma_start(out=v_raw[c][:], in_=v_view[:, 2 * c:2 * (c + 1), :, :])
-        load_pair(a_raw, a_view, 2)
-        load_pair(a_raw, a_view, 3)
+        load(a_raw, a_view, 4, 6)
+        load(a_raw, a_view, 6, 8)
 
         def copy_out(engine, dst, src):
             if engine == "scalar":
@@ -93,15 +99,34 @@ def tile_attention_prop_pb_kernel(tc, A, qe1, ke1, ve1, out):
             else:
                 nc.vector.tensor_copy(out=dst, in_=src)
 
-        def flip_pair(raw, grouped, a, banks, tag, engine):
-            planes = banks.tile([P, 2, 2, P], F32, tag=tag, name="planes")
-            for j in range(2):
-                words = raw[a][:, j, :].bitcast(F32)
+        def flip(rows, grouped, lo, banks, tag, engine, order):
+            n = len(rows)
+            planes = banks.tile([P, n, 2, P], F32, tag=tag, name="planes")
+            for j in range(n):
+                words = rows[j].bitcast(F32)
                 for u in range(2):
                     nc.tensor.transpose(planes[:, j, u, :], words[:, u * P:(u + 1) * P], ident_f32[:])
-            dst = grouped[:, a * 2 * P * PACK:(a + 1) * 2 * P * PACK].bitcast(F32)
-            copy_out(engine, dst.rearrange("p (j r u) -> p j r u", j=2, u=2),
-                     planes[:].rearrange("p j u r -> p j r u"))
+            dst = grouped[:, lo * PACK:(lo + n * P) * PACK].bitcast(F32)
+            if order == "run by run":
+                copy_out(engine, dst.rearrange("p (j r u) -> p j r u", j=n, u=2),
+                         planes[:].rearrange("p j u r -> p j r u"))
+            else:
+                copy_out(engine, dst.rearrange("p (r j u) -> p r j u", j=n, u=2),
+                         planes[:].rearrange("p j u r -> p r j u"))
+
+        def flip_k(a):
+            flip([k_raw[:, a, j, :] for j in range(2)], k_grouped, a * 2 * P, flip_banks, "flip", "scalar",
+                 "row by row")
+
+        def quantise_k(a):
+            quantise(k_grouped, k_codes, k_scales, a * 2 * P, (a + 1) * 2 * P)
+
+        def flip_q(lo, hi):
+            flip([q_raw[:, i, :] for i in range(lo, hi)], q_grouped, lo * P, out_banks, "out", "scalar",
+                 "run by run")
+
+        def quantise_q(lo, hi):
+            quantise(q_grouped, q_codes, q_scales, lo * P, hi * P)
 
         def quantise(grouped, codes, scales, lo, hi):
             nc.vector.quantize_mx(
@@ -138,17 +163,32 @@ def tile_attention_prop_pb_kernel(tc, A, qe1, ke1, ve1, out):
             i, h = divmod(n, 2)
             nc.vector.scalar_tensor_tensor(
                 out=masked[i][:, h * HALF:(h + 1) * HALF], in0=in_psum["scores", n][:],
-                scalar=INV_SQRT_F, in1=a_raw[i // 2][:, i % 2, h * HALF:(h + 1) * HALF],
+                scalar=INV_SQRT_F, in1=a_raw[:, i, h * HALF:(h + 1) * HALF],
                 op0=ALU.mult, op1=ALU.mult)
+
+        def lift_scores(n):
+            nc.scalar.activation(
+                out=lifted[n][:], in_=in_psum["scores", n][:], func=ACT.Copy, scale=INV_SQRT_F)
+
+        def mask_product_gpsimd(n):
+            i, h = divmod(n, 2)
+            for x in range(0, HALF, MASK_PIECE):
+                cols = slice(h * HALF + x, h * HALF + x + MASK_PIECE)
+                nc.gpsimd.tensor_tensor(
+                    out=masked[i][:, cols], in0=lifted[n][:, x:x + MASK_PIECE],
+                    in1=a_raw[:, i, cols], op=ALU.mult)
 
         def negative_row_max(i):
             nc.vector.tensor_reduce(
                 out=neg_max[i][:], in_=masked[i][:], axis=mybir.AxisListType.X, op=ALU.max, negate=True)
 
-        def exponentials(i):
+        def exponentials(i, half=None):
+            cols, total = slice(0, NK), e_sum[:, i:i + 1]
+            if half is not None:
+                cols, total = slice(half * HALF, (half + 1) * HALF), half_sum[:, half:half + 1]
             nc.scalar.activation(
-                out=e_rows[i][:], in_=masked[i][:], func=ACT.Exp, bias=neg_max[i][:], scale=1.0,
-                accum_out=e_sum[:, i:i + 1])
+                out=e_rows[i][:, cols], in_=masked[i][:, cols], func=ACT.Exp, bias=neg_max[i][:], scale=1.0,
+                accum_out=total)
 
         def transpose_e(i, banks):
             words = e_rows[i][:].bitcast(F32)
@@ -176,12 +216,8 @@ def tile_attention_prop_pb_kernel(tc, A, qe1, ke1, ve1, out):
         def reciprocals(g):
             nc.vector.reciprocal(inv_sum[g][:], e_sum[:, g * (QT // 2):(g + 1) * (QT // 2)])
 
-        def second_stage(i):
-            quantise_e(i)
-            second_matmul(i)
-
-        def second_matmul(i):
-            bank = out_banks.tile([P, F], F32, tag="out", name="out_bank")
+        def second_matmul(i, banks, tag):
+            bank = banks.tile([P, F], F32, tag=tag, name="out_bank")
             for c in range(2):
                 nc.tensor.matmul_mx(
                     out=bank[:],
@@ -195,85 +231,104 @@ def tile_attention_prop_pb_kernel(tc, A, qe1, ke1, ve1, out):
         def output(i, engine):
             g, j = divmod(i, QT // 2)
             inv = inv_sum[g][:, j:j + 1]
-            if engine == "scalar":
-                nc.scalar.activation(
-                    out=result[i][:], in_=in_psum["out", i][:], func=ACT.Copy, scale=inv)
-            else:
-                nc.vector.tensor_scalar(
-                    out=result[i][:], in0=in_psum["out", i][:], scalar1=inv, scalar2=None,
-                    op0=ALU.mult)
-            nc.sync.dma_start(out=o_view[:, i, :], in_=result[i][:])
+            halves = 2 if engine == "both" else 1
+            for x in range(halves):
+                cols = slice(x * F // halves, (x + 1) * F // halves)
+                if engine == "scalar" or (engine == "both" and x == 1):
+                    nc.scalar.activation(
+                        out=result[i][:, cols], in_=in_psum["out", i][:, cols], func=ACT.Copy, scale=inv)
+                else:
+                    nc.vector.tensor_scalar(
+                        out=result[i][:, cols], in0=in_psum["out", i][:, cols], scalar1=inv, scalar2=None,
+                        op0=ALU.mult)
+                nc.sync.dma_start(out=o_view[:, i, cols], in_=result[i][:, cols])
 
-        def flip_q(a):
-            flip_pair(q_raw, q_grouped, a, out_banks, "out", "scalar")
-
-        def quantise_q(a):
-            quantise(q_grouped, q_codes, q_scales, a * 2 * P, (a + 1) * 2 * P)
-
-        flip_q(0)
-        quantise_q(0)
+        flip_q(0, 1)
+        quantise_q(0, 1)
         for a in range(PAIRS):
-            flip_pair(k_raw, k_grouped, a, flip_banks, "flip", "scalar")
-            quantise(k_grouped, k_codes, k_scales, a * 2 * P, (a + 1) * 2 * P)
+            flip_k(a)
+            quantise_k(a)
         scores(0)
-        scores(2)
+        flip_q(1, 2)
         scores(1)
+        mask_product(0)
+        quantise_q(1, 2)
+        mask_product(1)
+        flip_q(2, 4)
+        scores(2)
+        scores(3)
+        lift_scores(3)
+        mask_product_gpsimd(3)
+        quantise_q(2, 4)
+        mask_product(2)
+        negative_row_max(0)
+        flip_q(4, 6)
+        flip_q(6, 8)
+        exponentials(0)
+        for n in (4, 5, 6):
+            scores(n)
+        mask_product(4)
+        mask_product(5)
+        quantise_q(4, 6)
+        negative_row_max(1)
+        quantise_q(6, 8)
         for c in range(2):
             regroup_v(c)
-        mask_product(0)
-        scores(3)
-        for a in range(1, PAIRS):
-            flip_q(a)
-        mask_product(2)
-        mask_product(1)
+        exponentials(1)
+        transpose_e(0, 1)
+        regroup_e(0, ("scalar",))
+        scores(7)
+        transpose_e(1, 1)
 
         last = QT - 1
-        for s in range(last):
+        for s in range(2, last):
             late = s - SECOND_STAGE_LAG
-            if s >= 2:
-                for n in (2 * s, 2 * s + 1):
+            for n in (2 * s, 2 * s + 1):
+                if n not in (4, 5) and n not in LIFTED:
                     mask_product(n)
-                    scores(n + SCORES_AHEAD)
-            if s + 1 < PAIRS:
-                quantise_q(s + 1)
+                scores(n + SCORES_AHEAD)
             if late == 0:
                 for c in range(2):
                     quantise_v(c)
             if late >= 0:
-                second_stage(late)
+                quantise_e(late)
+                second_matmul(late, out_banks, "out")
             negative_row_max(s)
-            if s == 0:
-                scores(4)
-                scores(5)
-                mask_product(3)
-                scores(6)
             if late == 0:
                 reciprocals(0)
             exponentials(s)
-            if s >= 1:
-                regroup_e(s - 1, ("scalar",))
+            if 2 * s + 5 in LIFTED:
+                lift_scores(2 * s + 5)
+                mask_product_gpsimd(2 * s + 5)
+            regroup_e(s - 1, ("scalar",))
             transpose_e(s, 1)
             if late >= 0:
                 output(late, "scalar")
 
-        left = list(range(last - SECOND_STAGE_LAG, last))
-        mask_product(2 * last)
-        mask_product(2 * last + 1)
-        second_stage(left[0])
+        for n in (2 * last, 2 * last + 1):
+            if n not in LIFTED:
+                mask_product(n)
+        quantise_e(3)
+        second_matmul(3, out_banks, "out")
         negative_row_max(last)
-        for j in left[1:OUT_BANKS]:
-            second_stage(j)
-        exponentials(last)
+        exponentials(last, 0)
+        exponentials(last, 1)
+        quantise_e(4)
+        second_matmul(4, out_banks, "out")
+        quantise_e(5)
         regroup_e(last - 1, ("vector",))
-        output(left[0], "scalar")
-        reciprocals(1)
-        output(left[1], "scalar")
+        quantise_e(6)
+        output(3, "scalar")
         transpose_e(last, 2)
-        for j in left[OUT_BANKS:]:
-            second_stage(j)
+        nc.vector.tensor_tensor(
+            out=e_sum[:, last:last + 1], in0=half_sum[:, 0:1], in1=half_sum[:, 1:2], op=ALU.add)
+        reciprocals(1)
+        second_matmul(5, score_banks, "scores")
+        second_matmul(6, score_banks, "scores")
         regroup_e(last, ("vector", "scalar"))
         quantise_e(last)
-        for j, engine in zip(left[OUT_BANKS:], ("scalar", "vector")):
-            output(j, engine)
-        second_matmul(last)
-        output(last, "scalar")
+        second_matmul(last, score_banks, "scores")
+        output(4, "scalar")
+        output(5, "scalar")
+        output(6, "vector")
+        output(last, "both")

@@ -24,8 +24,6 @@ FLOPS = 2 * NQ * NK * F * 2
 INV_SQRT_F = 1.0 / math.sqrt(F)
 
 SCORES_AHEAD = 4
-LIFTED = (3,)
-MASK_PIECE = 512
 V_PIECE = 128
 SECOND_STAGE_LAG = 4
 OUT_BANKS = 2
@@ -57,7 +55,6 @@ def tile_attention_prop_pb_kernel(tc, A, qe1, ke1, ve1, out):
         k_scales = sbuf.tile([P, NK], U8, name="k_scales", align_bytes=64)
         v_scales = sbuf.tile([P, 2 * F], U8, name="v_scales", align_bytes=64)
         masked = [sbuf.tile([P, NK], F32, name="masked%d" % i) for i in range(QT)]
-        lifted = {n: sbuf.tile([P, HALF], F32, name="lifted%d" % n) for n in LIFTED}
         neg_max = [sbuf.tile([P, 1], F32, name="neg_max%d" % i) for i in range(QT)]
         e_rows = [sbuf.tile([P, NK], BF16, name="e_rows%d" % i) for i in range(QT)]
         e_sum = sbuf.tile([P, QT], F32, name="e_sum")
@@ -71,7 +68,7 @@ def tile_attention_prop_pb_kernel(tc, A, qe1, ke1, ve1, out):
         in_psum = {}
 
         q_view = qe1.rearrange("(p i) f -> p i f", i=QT)
-        k_view = ke1.rearrange("(a p i) f -> p a i f", p=P, i=2)
+        k_view = ke1.rearrange("(a i p) f -> p a i f", p=P, i=2)
         a_view = A.rearrange("(p i) k -> p i k", i=QT)
         v_view = ve1.rearrange("(b p e) f -> p b e f", p=P, e=2)
         o_view = out.rearrange("(p i) f -> p i f", i=QT)
@@ -99,7 +96,7 @@ def tile_attention_prop_pb_kernel(tc, A, qe1, ke1, ve1, out):
             else:
                 nc.vector.tensor_copy(out=dst, in_=src)
 
-        def flip(rows, grouped, lo, banks, tag, engine, order):
+        def flip(rows, grouped, lo, banks, tag, engine):
             n = len(rows)
             planes = banks.tile([P, n, 2, P], F32, tag=tag, name="planes")
             for j in range(n):
@@ -107,23 +104,17 @@ def tile_attention_prop_pb_kernel(tc, A, qe1, ke1, ve1, out):
                 for u in range(2):
                     nc.tensor.transpose(planes[:, j, u, :], words[:, u * P:(u + 1) * P], ident_f32[:])
             dst = grouped[:, lo * PACK:(lo + n * P) * PACK].bitcast(F32)
-            if order == "run by run":
-                copy_out(engine, dst.rearrange("p (j r u) -> p j r u", j=n, u=2),
-                         planes[:].rearrange("p j u r -> p j r u"))
-            else:
-                copy_out(engine, dst.rearrange("p (r j u) -> p r j u", j=n, u=2),
-                         planes[:].rearrange("p j u r -> p r j u"))
+            copy_out(engine, dst.rearrange("p (j r u) -> p j r u", j=n, u=2),
+                     planes[:].rearrange("p j u r -> p j r u"))
 
         def flip_k(a):
-            flip([k_raw[:, a, j, :] for j in range(2)], k_grouped, a * 2 * P, flip_banks, "flip", "scalar",
-                 "row by row")
+            flip([k_raw[:, a, j, :] for j in range(2)], k_grouped, a * 2 * P, flip_banks, "flip", "scalar")
 
         def quantise_k(a):
             quantise(k_grouped, k_codes, k_scales, a * 2 * P, (a + 1) * 2 * P)
 
         def flip_q(lo, hi):
-            flip([q_raw[:, i, :] for i in range(lo, hi)], q_grouped, lo * P, out_banks, "out", "scalar",
-                 "run by run")
+            flip([q_raw[:, i, :] for i in range(lo, hi)], q_grouped, lo * P, out_banks, "out", "scalar")
 
         def quantise_q(lo, hi):
             quantise(q_grouped, q_codes, q_scales, lo * P, hi * P)
@@ -165,18 +156,6 @@ def tile_attention_prop_pb_kernel(tc, A, qe1, ke1, ve1, out):
                 out=masked[i][:, h * HALF:(h + 1) * HALF], in0=in_psum["scores", n][:],
                 scalar=INV_SQRT_F, in1=a_raw[:, i, h * HALF:(h + 1) * HALF],
                 op0=ALU.mult, op1=ALU.mult)
-
-        def lift_scores(n):
-            nc.scalar.activation(
-                out=lifted[n][:], in_=in_psum["scores", n][:], func=ACT.Copy, scale=INV_SQRT_F)
-
-        def mask_product_gpsimd(n):
-            i, h = divmod(n, 2)
-            for x in range(0, HALF, MASK_PIECE):
-                cols = slice(h * HALF + x, h * HALF + x + MASK_PIECE)
-                nc.gpsimd.tensor_tensor(
-                    out=masked[i][:, cols], in0=lifted[n][:, x:x + MASK_PIECE],
-                    in1=a_raw[:, i, cols], op=ALU.mult)
 
         def negative_row_max(i):
             nc.vector.tensor_reduce(
@@ -257,21 +236,20 @@ def tile_attention_prop_pb_kernel(tc, A, qe1, ke1, ve1, out):
         flip_q(2, 4)
         scores(2)
         scores(3)
-        lift_scores(3)
-        mask_product_gpsimd(3)
         quantise_q(2, 4)
         mask_product(2)
         negative_row_max(0)
+        mask_product(3)
         flip_q(4, 6)
         flip_q(6, 8)
         exponentials(0)
         for n in (4, 5, 6):
             scores(n)
+        quantise_q(4, 6)
+        quantise_q(6, 8)
+        negative_row_max(1)
         mask_product(4)
         mask_product(5)
-        quantise_q(4, 6)
-        negative_row_max(1)
-        quantise_q(6, 8)
         for c in range(2):
             regroup_v(c)
         exponentials(1)
@@ -284,7 +262,7 @@ def tile_attention_prop_pb_kernel(tc, A, qe1, ke1, ve1, out):
         for s in range(2, last):
             late = s - SECOND_STAGE_LAG
             for n in (2 * s, 2 * s + 1):
-                if n not in (4, 5) and n not in LIFTED:
+                if s > 2:
                     mask_product(n)
                 scores(n + SCORES_AHEAD)
             if late == 0:
@@ -297,17 +275,13 @@ def tile_attention_prop_pb_kernel(tc, A, qe1, ke1, ve1, out):
             if late == 0:
                 reciprocals(0)
             exponentials(s)
-            if 2 * s + 5 in LIFTED:
-                lift_scores(2 * s + 5)
-                mask_product_gpsimd(2 * s + 5)
             regroup_e(s - 1, ("scalar",))
             transpose_e(s, 1)
             if late >= 0:
                 output(late, "scalar")
 
         for n in (2 * last, 2 * last + 1):
-            if n not in LIFTED:
-                mask_product(n)
+            mask_product(n)
         quantise_e(3)
         second_matmul(3, out_banks, "out")
         negative_row_max(last)

@@ -40,6 +40,8 @@ def tile_attention_prop_pb_kernel(tc, A, qe1, ke1, ve1, out):
 
         ident_f32 = sbuf.tile([P, P], F32, name="ident_f32")
         make_identity(nc, ident_f32[:])
+        zeros = sbuf.tile([P, HALF], BF16, name="zeros")
+        nc.vector.memset(zeros[:], 0.0)
 
         q_raw = sbuf.tile([P, QT, F], BF16, name="q_raw")
         k_raw = sbuf.tile([P, PAIRS, 2, F], BF16, name="k_raw")
@@ -90,6 +92,12 @@ def tile_attention_prop_pb_kernel(tc, A, qe1, ke1, ve1, out):
         load(a_raw, a_view, 4, 6)
         load(a_raw, a_view, 6, 8)
 
+        warm_bank = score_banks.tile([P, HALF], F32, tag="scores", name="warm_bank")
+
+        def warm(times):
+            for repeat in range(times):
+                nc.tensor.matmul(warm_bank[:], lhsT=zeros[:, :P], rhs=zeros[:], start=True, stop=True)
+
         def copy_out(engine, dst, src):
             if engine == "scalar":
                 nc.scalar.copy(out=dst, in_=src)
@@ -108,7 +116,8 @@ def tile_attention_prop_pb_kernel(tc, A, qe1, ke1, ve1, out):
                      planes[:].rearrange("p j u r -> p j r u"))
 
         def flip_k(a):
-            flip([k_raw[:, a, j, :] for j in range(2)], k_grouped, a * 2 * P, flip_banks, "flip", "scalar")
+            banks, tag = ((flip_banks, "flip"), (out_banks, "out"))[a % 2]
+            flip([k_raw[:, a, j, :] for j in range(2)], k_grouped, a * 2 * P, banks, tag, "scalar")
 
         def quantise_k(a):
             quantise(k_grouped, k_codes, k_scales, a * 2 * P, (a + 1) * 2 * P)
@@ -222,10 +231,12 @@ def tile_attention_prop_pb_kernel(tc, A, qe1, ke1, ve1, out):
                         op0=ALU.mult)
                 nc.sync.dma_start(out=o_view[:, i, cols], in_=result[i][:, cols])
 
+        warm(4)
         flip_q(0, 1)
         quantise_q(0, 1)
         for a in range(PAIRS):
             flip_k(a)
+            warm(1)
             quantise_k(a)
         scores(0)
         flip_q(1, 2)

@@ -244,37 +244,35 @@ def tile_attention_prop_pb_kernel(tc, A, qe1, ke1, ve1, out):
         mask_product(0)
         quantise_q(1, 2)
         mask_product(1)
-        flip_q(2, 4)
         scores(2)
         scores(3)
-        quantise_q(2, 4)
+        flip_q(2, 4)
         mask_product(2)
         negative_row_max(0)
+        quantise_q(2, 4)
         mask_product(3)
         flip_q(4, 6)
         flip_q(6, 8)
         exponentials(0)
         for n in (4, 5, 6):
             scores(n)
-        quantise_q(4, 6)
-        quantise_q(6, 8)
+        quantise_q(4, 8)
         negative_row_max(1)
         mask_product(4)
-        mask_product(5)
         for c in range(2):
             regroup_v(c)
         exponentials(1)
         transpose_e(0, 1)
         regroup_e(0, ("scalar",))
         scores(7)
+        scores(8)
         transpose_e(1, 1)
 
         last = QT - 1
         for s in range(2, last):
             late = s - SECOND_STAGE_LAG
-            for n in (2 * s, 2 * s + 1):
-                if s > 2:
-                    mask_product(n)
+            for n in (2 * s + 1, 2 * s + 2):
+                mask_product(n)
                 scores(n + SCORES_AHEAD)
             if late == 0:
                 for c in range(2):
@@ -291,8 +289,7 @@ def tile_attention_prop_pb_kernel(tc, A, qe1, ke1, ve1, out):
             if late >= 0:
                 output(late, "scalar")
 
-        for n in (2 * last, 2 * last + 1):
-            mask_product(n)
+        mask_product(2 * last + 1)
         quantise_e(3)
         second_matmul(3, out_banks, "out")
         negative_row_max(last)

@@ -24,6 +24,7 @@ FLOPS = 2 * NQ * NK * F * 2
 INV_SQRT_F = 1.0 / math.sqrt(F)
 
 SCORES_AHEAD = 4
+LIFTED = (11,)
 V_PIECE = 128
 SECOND_STAGE_LAG = 4
 OUT_BANKS = 2
@@ -57,6 +58,7 @@ def tile_attention_prop_pb_kernel(tc, A, qe1, ke1, ve1, out):
         k_scales = sbuf.tile([P, NK], U8, name="k_scales", align_bytes=64)
         v_scales = sbuf.tile([P, 2 * F], U8, name="v_scales", align_bytes=64)
         masked = [sbuf.tile([P, NK], F32, name="masked%d" % i) for i in range(QT)]
+        lifted = {n: sbuf.tile([P, HALF], F32, name="lifted%d" % n) for n in LIFTED}
         neg_max = [sbuf.tile([P, 1], F32, name="neg_max%d" % i) for i in range(QT)]
         e_rows = [sbuf.tile([P, NK], BF16, name="e_rows%d" % i) for i in range(QT)]
         e_sum = sbuf.tile([P, QT], F32, name="e_sum")
@@ -166,6 +168,16 @@ def tile_attention_prop_pb_kernel(tc, A, qe1, ke1, ve1, out):
                 scalar=INV_SQRT_F, in1=a_raw[:, i, h * HALF:(h + 1) * HALF],
                 op0=ALU.mult, op1=ALU.mult)
 
+        def lift_scores(n):
+            nc.scalar.activation(
+                out=lifted[n][:], in_=in_psum["scores", n][:], func=ACT.Copy, scale=INV_SQRT_F)
+
+        def mask_product_gpsimd(n):
+            i, h = divmod(n, 2)
+            nc.gpsimd.tensor_tensor(
+                out=masked[i][:, h * HALF:(h + 1) * HALF], in0=lifted[n][:],
+                in1=a_raw[:, i, h * HALF:(h + 1) * HALF], op=ALU.mult)
+
         def negative_row_max(i):
             nc.vector.tensor_reduce(
                 out=neg_max[i][:], in_=masked[i][:], axis=mybir.AxisListType.X, op=ALU.max, negate=True)
@@ -272,7 +284,8 @@ def tile_attention_prop_pb_kernel(tc, A, qe1, ke1, ve1, out):
         for s in range(2, last):
             late = s - SECOND_STAGE_LAG
             for n in (2 * s + 1, 2 * s + 2):
-                mask_product(n)
+                if n not in LIFTED:
+                    mask_product(n)
                 scores(n + SCORES_AHEAD)
             if late == 0:
                 for c in range(2):
@@ -285,11 +298,15 @@ def tile_attention_prop_pb_kernel(tc, A, qe1, ke1, ve1, out):
                 reciprocals(0)
             exponentials(s)
             regroup_e(s - 1, ("scalar",))
+            if 2 * s + 5 in LIFTED:
+                lift_scores(2 * s + 5)
+                mask_product_gpsimd(2 * s + 5)
             transpose_e(s, 1)
             if late >= 0:
                 output(late, "scalar")
 
-        mask_product(2 * last + 1)
+        if 2 * last + 1 not in LIFTED:
+            mask_product(2 * last + 1)
         quantise_e(3)
         second_matmul(3, out_banks, "out")
         negative_row_max(last)

from contextlib import ExitStack
import math

import concourse.mybir as mybir
from concourse.masks import make_identity

FP8X4 = mybir.dt.float8_e4m3fn_x4
BF16 = mybir.dt.bfloat16
F32 = mybir.dt.float32
U32 = mybir.dt.uint32
U8 = mybir.dt.uint8
ALU = mybir.AluOpType
ACT = mybir.ActivationFunctionType

P = 128
PACK = 4
NQ = 1024
NK = 1024
F = 512
QT = NQ // P
HALF = 512
PAIRS = 4
FLOPS = 2 * NQ * NK * F * 2
INV_SQRT_F = 1.0 / math.sqrt(F)

SCORES_AHEAD = 4
LIFTED = (11,)
V_PIECE = 128
SECOND_STAGE_LAG = 4
OUT_BANKS = 2


def tile_attention_prop_pb_kernel(tc, A, qe1, ke1, ve1, out):
    nc = tc.nc
    with ExitStack() as ctx:
        sbuf = ctx.enter_context(tc.tile_pool(name="sbuf", bufs=1))
        score_banks = ctx.enter_context(tc.psum_pool(name="score_banks", bufs=SCORES_AHEAD))
        flip_banks = ctx.enter_context(tc.psum_pool(name="flip_banks", bufs=2))
        out_banks = ctx.enter_context(tc.psum_pool(name="out_banks", bufs=OUT_BANKS))
        ctx.enter_context(tc.manual_schedule())

        ident_f32 = sbuf.tile([P, P], F32, name="ident_f32")
        make_identity(nc, ident_f32[:])
        zeros = sbuf.tile([P, HALF], BF16, name="zeros")
        nc.vector.memset(zeros[:], 0.0)

        q_raw = sbuf.tile([P, QT, F], BF16, name="q_raw")
        k_raw = sbuf.tile([P, PAIRS, 2, F], BF16, name="k_raw")
        a_raw = sbuf.tile([P, QT, NK], BF16, name="a_raw")
        v_raw = [sbuf.tile([P, 2, 2, F], BF16, name="v_raw%d" % c) for c in range(2)]
        q_grouped = sbuf.tile([P, NQ * PACK], BF16, name="q_grouped", align_bytes=64)
        k_grouped = sbuf.tile([P, NK * PACK], BF16, name="k_grouped", align_bytes=64)
        v_grouped = sbuf.tile([P, 2, F, PACK], BF16, name="v_grouped", align_bytes=64)
        q_codes = sbuf.tile([P, NQ], U32, name="q_codes", align_bytes=64)
        k_codes = sbuf.tile([P, NK], U32, name="k_codes", align_bytes=64)
        v_codes = sbuf.tile([P, 2 * F], U32, name="v_codes", align_bytes=64)
        q_scales = sbuf.tile([P, NQ], U8, name="q_scales", align_bytes=64)
        k_scales = sbuf.tile([P, NK], U8, name="k_scales", align_bytes=64)
        v_scales = sbuf.tile([P, 2 * F], U8, name="v_scales", align_bytes=64)
        masked = [sbuf.tile([P, NK], F32, name="masked%d" % i) for i in range(QT)]
        lifted = {n: sbuf.tile([P, HALF], F32, name="lifted%d" % n) for n in LIFTED}
        neg_max = [sbuf.tile([P, 1], F32, name="neg_max%d" % i) for i in range(QT)]
        e_rows = [sbuf.tile([P, NK], BF16, name="e_rows%d" % i) for i in range(QT)]
        e_sum = sbuf.tile([P, QT], F32, name="e_sum")
        e_grouped = [
            sbuf.tile([P, 2, P, PACK], BF16, name="e_grouped%d" % i, align_bytes=64) for i in range(QT)]
        e_codes = [sbuf.tile([P, 2 * P], U32, name="e_codes%d" % i, align_bytes=64) for i in range(QT)]
        e_scales = [sbuf.tile([P, 2 * P], U8, name="e_scales%d" % i, align_bytes=64) for i in range(QT)]
        half_sum = sbuf.tile([P, 2], F32, name="half_sum")
        inv_sum = [sbuf.tile([P, QT // 2], F32, name="inv_sum%d" % g) for g in range(2)]
        result = [sbuf.tile([P, F], F32, name="result%d" % i) for i in range(QT)]
        in_psum = {}

        q_view = qe1.rearrange("(p i) f -> p i f", i=QT)
        k_view = ke1.rearrange("(a i p) f -> p a i f", p=P, i=2)
        a_view = A.rearrange("(p i) k -> p i k", i=QT)
        v_view = ve1.rearrange("(b p e) f -> p b e f", p=P, e=2)
        o_view = out.rearrange("(p i) f -> p i f", i=QT)

        def load(raw, view, lo, hi):
            nc.sync.dma_start(out=raw[:, lo:hi], in_=view[:, lo:hi])

        load(q_raw, q_view, 0, 1)
        for a in range(PAIRS):
            load(k_raw, k_view, a, a + 1)
        load(a_raw, a_view, 0, 1)
        load(q_raw, q_view, 1, 2)
        load(q_raw, q_view, 2, 4)
        load(a_raw, a_view, 1, 2)
        load(q_raw, q_view, 4, 8)
        load(a_raw, a_view, 2, 4)
        for c in range(2):
            nc.sync.dma_start(out=v_raw[c][:], in_=v_view[:, 2 * c:2 * (c + 1), :, :])
        load(a_raw, a_view, 4, 6)
        load(a_raw, a_view, 6, 8)

        warm_bank = score_banks.tile([P, HALF], F32, tag="scores", name="warm_bank")

        def warm(times):
            for repeat in range(times):
                nc.tensor.matmul(warm_bank[:], lhsT=zeros[:, :P], rhs=zeros[:], start=True, stop=True)

        def copy_out(engine, dst, src):
            if engine == "scalar":
                nc.scalar.copy(out=dst, in_=src)
            else:
                nc.vector.tensor_copy(out=dst, in_=src)

        def flip(rows, grouped, lo, banks, tag, engine):
            n = len(rows)
            planes = banks.tile([P, n, 2, P], F32, tag=tag, name="planes")
            for j in range(n):
                words = rows[j].bitcast(F32)
                for u in range(2):
                    nc.tensor.transpose(planes[:, j, u, :], words[:, u * P:(u + 1) * P], ident_f32[:])
            dst = grouped[:, lo * PACK:(lo + n * P) * PACK].bitcast(F32)
            copy_out(engine, dst.rearrange("p (j r u) -> p j r u", j=n, u=2),
                     planes[:].rearrange("p j u r -> p j r u"))

        def flip_k(a):
            banks, tag = ((flip_banks, "flip"), (out_banks, "out"))[a % 2]
            flip([k_raw[:, a, j, :] for j in range(2)], k_grouped, a * 2 * P, banks, tag, "scalar")

        def quantise_k(a):
            quantise(k_grouped, k_codes, k_scales, a * 2 * P, (a + 1) * 2 * P)

        def flip_q(lo, hi):
            flip([q_raw[:, i, :] for i in range(lo, hi)], q_grouped, lo * P, out_banks, "out", "scalar")

        def quantise_q(lo, hi):
            quantise(q_grouped, q_codes, q_scales, lo * P, hi * P)

        def quantise(grouped, codes, scales, lo, hi):
            nc.vector.quantize_mx(
                out=codes[:, lo:hi].bitcast(FP8X4), scales=scales[:, lo:hi],
                in_=grouped[:, PACK * lo:PACK * hi])

        def regroup_v(c):
            for f in range(0, F, V_PIECE):
                nc.gpsimd.tensor_scalar(
                    out=v_grouped[:, c, f:f + V_PIECE, :],
                    in0=v_raw[c][:, :, :, f:f + V_PIECE].rearrange("p u e f -> p f (u e)"),
                    scalar1=1.0, scalar2=0.0, op0=ALU.mult, op1=ALU.add)

        def quantise_v(c):
            nc.vector.quantize_mx(
                out=v_codes[:, c * F:(c + 1) * F].bitcast(FP8X4), scales=v_scales[:, c * F:(c + 1) * F],
                in_=v_grouped[:, c, :, :].rearrange("p f t -> p (f t)"))

        def scores(n):
            if n >= 2 * QT:
                return
            i, h = divmod(n, 2)
            bank = score_banks.tile([P, HALF], F32, tag="scores", name="bank")
            nc.tensor.matmul_mx(
                out=bank[:],
                lhsT=q_codes[:, i * P:(i + 1) * P].bitcast(FP8X4),
                lhsT_scale=q_scales[:, i * P:(i + 1) * P],
                rhs=k_codes[:, h * HALF:(h + 1) * HALF].bitcast(FP8X4),
                rhs_scale=k_scales[:, h * HALF:(h + 1) * HALF],
                start=True, stop=True)
            in_psum["scores", n] = bank

        def mask_product(n):
            i, h = divmod(n, 2)
            nc.vector.scalar_tensor_tensor(
                out=masked[i][:, h * HALF:(h + 1) * HALF], in0=in_psum["scores", n][:],
                scalar=INV_SQRT_F, in1=a_raw[:, i, h * HALF:(h + 1) * HALF],
                op0=ALU.mult, op1=ALU.mult)

        def lift_scores(n):
            nc.scalar.activation(
                out=lifted[n][:], in_=in_psum["scores", n][:], func=ACT.Copy, scale=INV_SQRT_F)

        def mask_product_gpsimd(n):
            i, h = divmod(n, 2)
            nc.gpsimd.tensor_tensor(
                out=masked[i][:, h * HALF:(h + 1) * HALF], in0=lifted[n][:],
                in1=a_raw[:, i, h * HALF:(h + 1) * HALF], op=ALU.mult)

        def negative_row_max(i):
            nc.vector.tensor_reduce(
                out=neg_max[i][:], in_=masked[i][:], axis=mybir.AxisListType.X, op=ALU.max, negate=True)

        def exponentials(i, half=None):
            cols, total = slice(0, NK), e_sum[:, i:i + 1]
            if half is not None:
                cols, total = slice(half * HALF, (half + 1) * HALF), half_sum[:, half:half + 1]
            nc.scalar.activation(
                out=e_rows[i][:, cols], in_=masked[i][:, cols], func=ACT.Exp, bias=neg_max[i][:], scale=1.0,
                accum_out=total)

        def transpose_e(i, banks):
            words = e_rows[i][:].bitcast(F32)
            share = 2 // banks
            for g in range(banks):
                planes = flip_banks.tile([P, share, 2, P], F32, tag="flip", name="e_planes")
                for j in range(share):
                    for u in range(2):
                        b = 2 * (g * share + j) + u
                        nc.tensor.transpose(planes[:, j, u, :], words[:, b * P:(b + 1) * P], ident_f32[:])
                in_psum["e", i, g] = planes

        def regroup_e(i, engines):
            share = 2 // len(engines)
            for g, engine in enumerate(engines):
                dst = e_grouped[i][:, g * share:(g + 1) * share, :, :].rearrange("p c r t -> p (c r t)").bitcast(F32)
                copy_out(engine, dst.rearrange("p (c r u) -> p c r u", c=share, u=2),
                         in_psum["e", i, g][:].rearrange("p c u r -> p c r u"))

        def quantise_e(i):
            nc.vector.quantize_mx(
                out=e_codes[i][:].bitcast(FP8X4), scales=e_scales[i][:],
                in_=e_grouped[i][:].rearrange("p c r t -> p (c r t)"))

        def reciprocals(g):
            nc.vector.reciprocal(inv_sum[g][:], e_sum[:, g * (QT // 2):(g + 1) * (QT // 2)])

        def second_matmul(i, banks, tag):
            bank = banks.tile([P, F], F32, tag=tag, name="out_bank")
            for c in range(2):
                nc.tensor.matmul_mx(
                    out=bank[:],
                    lhsT=e_codes[i][:, c * P:(c + 1) * P].bitcast(FP8X4),
                    lhsT_scale=e_scales[i][:, c * P:(c + 1) * P],
                    rhs=v_codes[:, c * F:(c + 1) * F].bitcast(FP8X4),
                    rhs_scale=v_scales[:, c * F:(c + 1) * F],
                    start=(c == 0), stop=(c == 1))
            in_psum["out", i] = bank

        def output(i, engine):
            g, j = divmod(i, QT // 2)
            inv = inv_sum[g][:, j:j + 1]
            halves = 2 if engine == "both" else 1
            for x in range(halves):
                cols = slice(x * F // halves, (x + 1) * F // halves)
                if engine == "scalar" or (engine == "both" and x == 1):
                    nc.scalar.activation(
                        out=result[i][:, cols], in_=in_psum["out", i][:, cols], func=ACT.Copy, scale=inv)
                else:
                    nc.vector.tensor_scalar(
                        out=result[i][:, cols], in0=in_psum["out", i][:, cols], scalar1=inv, scalar2=None,
                        op0=ALU.mult)
                nc.sync.dma_start(out=o_view[:, i, cols], in_=result[i][:, cols])

        warm(4)
        flip_q(0, 1)
        quantise_q(0, 1)
        for a in range(PAIRS):
            flip_k(a)
            warm(1)
            quantise_k(a)
        scores(0)
        flip_q(1, 2)
        scores(1)
        mask_product(0)
        quantise_q(1, 2)
        mask_product(1)
        scores(2)
        scores(3)
        flip_q(2, 4)
        mask_product(2)
        negative_row_max(0)
        quantise_q(2, 4)
        mask_product(3)
        flip_q(4, 6)
        flip_q(6, 8)
        exponentials(0)
        for n in (4, 5, 6):
            scores(n)
        quantise_q(4, 8)
        negative_row_max(1)
        mask_product(4)
        for c in range(2):
            regroup_v(c)
        exponentials(1)
        transpose_e(0, 1)
        regroup_e(0, ("scalar",))
        scores(7)
        scores(8)
        transpose_e(1, 1)

        last = QT - 1
        for s in range(2, last):
            late = s - SECOND_STAGE_LAG
            for n in (2 * s + 1, 2 * s + 2):
                if n not in LIFTED:
                    mask_product(n)
                scores(n + SCORES_AHEAD)
            if late == 0:
                for c in range(2):
                    quantise_v(c)
            if late >= 0:
                quantise_e(late)
                second_matmul(late, out_banks, "out")
            negative_row_max(s)
            if late == 0:
                reciprocals(0)
            exponentials(s)
            regroup_e(s - 1, ("scalar",))
            if 2 * s + 5 in LIFTED:
                lift_scores(2 * s + 5)
                mask_product_gpsimd(2 * s + 5)
            transpose_e(s, 1)
            if late >= 0:
                output(late, "scalar")

        if 2 * last + 1 not in LIFTED:
            mask_product(2 * last + 1)
        quantise_e(3)
        second_matmul(3, out_banks, "out")
        negative_row_max(last)
        exponentials(last, 0)
        exponentials(last, 1)
        quantise_e(4)
        second_matmul(4, out_banks, "out")
        quantise_e(5)
        regroup_e(last - 1, ("vector",))
        quantise_e(6)
        output(3, "scalar")
        transpose_e(last, 2)
        nc.vector.tensor_tensor(
            out=e_sum[:, last:last + 1], in0=half_sum[:, 0:1], in1=half_sum[:, 1:2], op=ALU.add)
        reciprocals(1)
        second_matmul(5, score_banks, "scores")
        second_matmul(6, score_banks, "scores")
        regroup_e(last, ("vector", "scalar"))
        quantise_e(last)
        second_matmul(last, score_banks, "scores")
        output(4, "scalar")
        output(5, "scalar")
        output(6, "vector")
        output(last, "both")
